import numpy as np
import ml_dtypes


def mxq(x, axis, fmt="e4m3"):
    dtype, down = {"e4m3": (ml_dtypes.float8_e4m3fn, 7), "e5m2": (ml_dtypes.float8_e5m2, 14)}[fmt]
    v = np.moveaxis(np.asarray(x, np.float32).astype(ml_dtypes.bfloat16).astype(np.float64), axis, -1)
    blocks = v.reshape(v.shape[:-1] + (-1, 32))
    amax = np.abs(blocks).max(-1, keepdims=True)
    byte = np.maximum(np.where(amax > 0, np.frexp(amax)[1] - 1 + 127, 0) - down, 1)
    scale = np.exp2(byte - 127.0)
    codes = (blocks / scale).astype(np.float32).astype(dtype).astype(np.float64)
    return np.moveaxis((codes * scale).reshape(v.shape), -1, axis)


WIDE = False


def mx_kscale(k):
    if not WIDE:
        return np.ones(k)
    levels = np.array([20, -20, 10, -10, 0])
    a = np.random.permutation(np.resize(levels, k // 512 * 4)).reshape(k // 512, 4)
    idx = np.arange(k)
    return np.exp2(a[idx // 512, idx % 128 // 32])


BF16 = ml_dtypes.bfloat16


def bf(x):
    return np.asarray(x, np.float32).astype(BF16)


def f64(x):
    return np.asarray(x).astype(np.float64)


BS, P, C, D, E = 2048, 128, 32, 16, 8
K = P * E
N = C * D


def setup_inputs():
    u = mx_kscale(N).reshape(C, D)
    x = bf(np.random.standard_normal((BS, P, E)))
    W0 = bf(np.random.standard_normal((1, P, C, D, E)) * np.sqrt(P / E))
    g = bf(np.random.standard_normal((BS, C, D, 1)) * np.exp2(np.random.randint(-12, 1, (BS, 1, 1, 1))) * 32.0 * u[None, :, :, None])
    wf0 = f64(W0)[0].transpose(0, 3, 1, 2).reshape(K, N)
    s = (f64(x).reshape(BS, K) @ wf0).reshape(BS, C, D) / P
    W = bf(f64(W0) / u[None, None, :, :, None])
    return {"x": x, "W": W, "s": np.asarray(s, np.float32), "grad_out": g}


def reference(x, W, s, grad_out):
    sf = f64(s)
    ds = f64(grad_out)[..., 0] * (2.0 * np.abs(sf) / np.square(1.0 + sf * sf))
    ds = ds.reshape(BS, N)
    wf = f64(W)[0].transpose(0, 3, 1, 2).reshape(K, N)
    gx = (mxq(ds, 1, "e5m2") @ mxq(wf, 1, "e4m3").T) / P
    return gx.reshape(BS, P, E)

@@ -1,0 +1,166 @@
+import concourse.mybir as mybir
+from concourse.masks import make_identity
+
+F32 = mybir.dt.float32
+BF16 = mybir.dt.bfloat16
+U32 = mybir.dt.uint32
+U8 = mybir.dt.uint8
+E4M3_X4 = mybir.dt.float8_e4m3fn_x4
+E5M2_X4 = mybir.dt.float8_e5m2_x4
+ACT = mybir.ActivationFunctionType
+ALU = mybir.AluOpType
+
+P = 128
+PACK = 4
+ROWS = 2048
+N = 512
+K = 1024
+E_PAIRS = 4
+BLOCKS = ROWS // P
+GROUP = 2
+GROUPS = BLOCKS // GROUP
+BANK = 512
+HALVES = K // BANK
+
+FLOPS = 2 * ROWS * K * N
+BYTES = 2 * K * N + 4 * ROWS * N + 2 * ROWS * N + 4 * ROWS * K
+
+
+def quantise_w(nc, const, psum, w_sb, ident_f32, w_codes, w_scales):
+    w_words = w_sb[:].bitcast(F32).rearrange("p (u i w) -> p u i w", u=PACK, i=P, w=E_PAIRS)
+    w_grouped = const.tile([P, P, E_PAIRS, 2, PACK], BF16, align_bytes=64)
+    for w in range(E_PAIRS):
+        w_ps = psum.tile([P, PACK, P], F32, tag="o_ps")
+        for u in range(PACK):
+            nc.tensor.transpose(w_ps[:, u, :], w_words[:, u, :, w], ident_f32[:])
+        nc.vector.tensor_copy(
+            out=w_grouped[:, :, w, :, :],
+            in_=w_ps[:].bitcast(BF16).rearrange("i u (p l) -> i p l u", l=2),
+        )
+    w_flat = w_grouped[:].rearrange("i p w l u -> i (p w l u)")
+    for h in range(HALVES):
+        nc.vector.quantize_mx(
+            out=w_codes[:, h * BANK : (h + 1) * BANK].bitcast(E4M3_X4),
+            scales=w_scales[:, h * BANK : (h + 1) * BANK],
+            in_=w_flat[:, h * BANK * PACK : (h + 1) * BANK * PACK],
+        )
+
+
+def tile_digitcaps_t_v_kernel(tc, x, W, s, grad_out, out):
+    nc = tc.nc
+    s_rows = s.rearrange("(p t) c d -> p t (c d)", t=BLOCKS)
+    g_rows = grad_out.rearrange("(p t) c d o -> p t (c d o)", t=BLOCKS)
+    out_rows = out.rearrange("(p t) q e -> p t (q e)", t=BLOCKS)
+    w_rows = W.rearrange("o p c d e -> (o p) (c d e)")
+
+    with (
+        tc.tile_pool(name="const", bufs=1) as const,
+        tc.tile_pool(name="work", bufs=3) as work,
+        tc.psum_pool(name="psum_t", bufs=2) as psum_t,
+        tc.psum_pool(name="psum_o", bufs=4) as psum_o,
+    ):
+        s_sb = [const.tile([P, GROUP, N], F32, name="s_sb%d" % j) for j in range(GROUPS)]
+        g_sb = [const.tile([P, GROUP, N], BF16, name="g_sb%d" % j) for j in range(GROUPS)]
+        w_sb = const.tile([P, N * 8], BF16)
+        for j in range(GROUPS):
+            blocks = slice(j * GROUP, (j + 1) * GROUP)
+            nc.sync.dma_start(out=s_sb[j][:], in_=s_rows[:, blocks, :])
+            if j == 0:
+                nc.sync.dma_start(out=w_sb[:], in_=w_rows)
+            nc.sync.dma_start(out=g_sb[j][:], in_=g_rows[:, blocks, :])
+
+        ident_f32 = const.tile([P, P], F32)
+        make_identity(nc, ident_f32[:])
+        ident_bf16 = const.tile([P, P], BF16)
+        make_identity(nc, ident_bf16[:])
+        one = const.tile([P, 1], F32)
+        nc.vector.memset(one[:], 1.0)
+        warm = const.tile([P, 1], F32)
+        nc.scalar.activation(out=warm[:], in_=one[:], func=ACT.Abs_reciprocal_sqrt)
+
+        w_codes = const.tile([P, K], U32, align_bytes=64)
+        w_scales = const.tile([P, K], U8, align_bytes=64)
+        quantise_w(nc, const, psum_o, w_sb, ident_f32, w_codes, w_scales)
+
+        for j in range(GROUPS):
+            s_flat = s_sb[j][:].rearrange("p t n -> p (t n)")
+
+            sq = work.tile([P, GROUP * N], F32)
+            nc.scalar.activation(out=sq[:], in_=s_flat, func=ACT.Square)
+            den = work.tile([P, GROUP * N], F32)
+            nc.scalar.activation(out=den[:], in_=sq[:], func=ACT.Square, bias=one[:])
+            c0 = work.tile([P, GROUP * N], F32)
+            nc.scalar.activation(out=c0[:], in_=den[:], func=ACT.Abs_reciprocal_sqrt)
+            tau = work.tile([P, GROUP * N], F32)
+            nc.vector.scalar_tensor_tensor(
+                out=tau[:], in0=sq[:], scalar=1.0, in1=c0[:], op0=ALU.add, op1=ALU.mult
+            )
+            c1 = work.tile([P, GROUP * N], F32)
+            nc.vector.scalar_tensor_tensor(
+                out=c1[:], in0=tau[:], scalar=2.0, in1=c0[:], op0=ALU.subtract, op1=ALU.mult
+            )
+            r = work.tile([P, GROUP * N], F32)
+            nc.scalar.activation(out=r[:], in_=c1[:], func=ACT.Square)
+            y = work.tile([P, GROUP, PACK, P], F32)
+            nc.gpsimd.tensor_tensor(
+                out=y[:].rearrange("p t u i -> p (t u i)"), in0=s_flat, in1=r[:], op=ALU.mult
+            )
+
+            g_ps = psum_t.tile([P, GROUP, PACK, P], BF16)
+            f = work.tile([P, GROUP, P, PACK], F32)
+            for t in range(GROUP):
+                y_ps = psum_t.tile([P, PACK, P], F32)
+                for u in range(PACK):
+                    nc.tensor.transpose(y_ps[:, u, :], y[:, t, u, :], ident_f32[:])
+                for u in range(PACK):
+                    nc.tensor.transpose(
+                        g_ps[:, t, u, :], g_sb[j][:, t, u * P : (u + 1) * P], ident_bf16[:]
+                    )
+                nc.scalar.activation(
+                    out=f[:, t, :, :],
+                    in_=y_ps[:].rearrange("i u b -> i b u"),
+                    func=ACT.Abs,
+                    scale=2.0,
+                )
+            ds = work.tile([P, GROUP, P, PACK], BF16, align_bytes=64)
+            for t in range(GROUP):
+                nc.vector.scalar_tensor_tensor(
+                    out=ds[:, t, :, :],
+                    in0=f[:, t, :, :],
+                    scalar=0.0,
+                    in1=g_ps[:, t, :, :].rearrange("i u b -> i b u"),
+                    op0=ALU.max,
+                    op1=ALU.mult,
+                )
+
+            ds_codes = work.tile([P, GROUP * P], U32, align_bytes=64)
+            ds_scales = work.tile([P, GROUP * P], U8, align_bytes=64)
+            nc.vector.quantize_mx(
+                out=ds_codes[:].bitcast(E5M2_X4),
+                scales=ds_scales[:],
+                in_=ds[:].rearrange("i t b u -> i (t b u)"),
+            )
+            o_sb = work.tile([P, GROUP, K], F32)
+            for t in range(GROUP):
+                rows = slice(t * P, (t + 1) * P)
+                for h in range(HALVES):
+                    cols = slice(h * BANK, (h + 1) * BANK)
+                    o_ps = psum_o.tile([P, BANK], F32)
+                    nc.tensor.matmul_mx(
+                        out=o_ps[:],
+                        lhsT=ds_codes[:, rows].bitcast(E5M2_X4),
+                        lhsT_scale=ds_scales[:, rows],
+                        rhs=w_codes[:, cols].bitcast(E4M3_X4),
+                        rhs_scale=w_scales[:, cols],
+                        start=True,
+                        stop=True,
+                    )
+                    if t == GROUP - 1 and h == HALVES - 1:
+                        nc.scalar.activation(
+                            out=o_sb[:, t, cols], in_=o_ps[:], func=ACT.Copy, scale=1.0 / P
+                        )
+                    else:
+                        nc.vector.tensor_scalar_mul(
+                            out=o_sb[:, t, cols], in0=o_ps[:], scalar1=1.0 / P
+                        )
+            nc.sync.dma_start(out=out_rows[:, j * GROUP : (j + 1) * GROUP, :], in_=o_sb[:])

@@ -21,6 +21,7 @@ GROUP = 2
 GROUPS = BLOCKS // GROUP
 BANK = 512
 HALVES = K // BANK
+LAG = 2
 
 FLOPS = 2 * ROWS * K * N
 BYTES = 2 * K * N + 4 * ROWS * N + 2 * ROWS * N + 4 * ROWS * K
@@ -56,6 +57,7 @@ def tile_digitcaps_t_v_kernel(tc, x, W, s, grad_out, out):
     with (
         tc.tile_pool(name="const", bufs=1) as const,
         tc.tile_pool(name="work", bufs=3) as work,
+        tc.tile_pool(name="ahead", bufs=LAG + 2) as ahead,
         tc.psum_pool(name="psum_t", bufs=2) as psum_t,
         tc.psum_pool(name="psum_o", bufs=4) as psum_o,
     ):
@@ -82,9 +84,8 @@ def tile_digitcaps_t_v_kernel(tc, x, W, s, grad_out, out):
         w_scales = const.tile([P, K], U8, align_bytes=64)
         quantise_w(nc, const, psum_o, w_sb, ident_f32, w_codes, w_scales)
 
-        for j in range(GROUPS):
+        def rows_on_partitions(j):
             s_flat = s_sb[j][:].rearrange("p t n -> p (t n)")
-
             sq = work.tile([P, GROUP * N], F32)
             nc.scalar.activation(out=sq[:], in_=s_flat, func=ACT.Square)
             den = work.tile([P, GROUP * N], F32)
@@ -101,11 +102,13 @@ def tile_digitcaps_t_v_kernel(tc, x, W, s, grad_out, out):
             )
             r = work.tile([P, GROUP * N], F32)
             nc.scalar.activation(out=r[:], in_=c1[:], func=ACT.Square)
-            y = work.tile([P, GROUP, PACK, P], F32)
+            y = ahead.tile([P, GROUP, PACK, P], F32)
             nc.gpsimd.tensor_tensor(
                 out=y[:].rearrange("p t u i -> p (t u i)"), in0=s_flat, in1=r[:], op=ALU.mult
             )
+            return y
 
+        def contraction_on_partitions(j, y):
             g_ps = psum_t.tile([P, GROUP, PACK, P], BF16)
             f = work.tile([P, GROUP, P, PACK], F32)
             for t in range(GROUP):
@@ -140,9 +143,9 @@ def tile_digitcaps_t_v_kernel(tc, x, W, s, grad_out, out):
                 scales=ds_scales[:],
                 in_=ds[:].rearrange("i t b u -> i (t b u)"),
             )
-            o_sb = work.tile([P, GROUP, K], F32)
             for t in range(GROUP):
                 rows = slice(t * P, (t + 1) * P)
+                o_sb = work.tile([P, K], F32)
                 for h in range(HALVES):
                     cols = slice(h * BANK, (h + 1) * BANK)
                     o_ps = psum_o.tile([P, BANK], F32)
@@ -155,12 +158,17 @@ def tile_digitcaps_t_v_kernel(tc, x, W, s, grad_out, out):
                         start=True,
                         stop=True,
                     )
-                    if t == GROUP - 1 and h == HALVES - 1:
+                    if j >= GROUPS // 2 and h == HALVES - 1:
                         nc.scalar.activation(
-                            out=o_sb[:, t, cols], in_=o_ps[:], func=ACT.Copy, scale=1.0 / P
+                            out=o_sb[:, cols], in_=o_ps[:], func=ACT.Copy, scale=1.0 / P
                         )
                     else:
-                        nc.vector.tensor_scalar_mul(
-                            out=o_sb[:, t, cols], in0=o_ps[:], scalar1=1.0 / P
-                        )
-            nc.sync.dma_start(out=out_rows[:, j * GROUP : (j + 1) * GROUP, :], in_=o_sb[:])
+                        nc.vector.tensor_scalar_mul(out=o_sb[:, cols], in0=o_ps[:], scalar1=1.0 / P)
+                nc.sync.dma_start(out=out_rows[:, j * GROUP + t, :], in_=o_sb[:])
+
+        y_of = {}
+        for j in range(GROUPS + LAG):
+            if j < GROUPS:
+                y_of[j] = rows_on_partitions(j)
+            if j >= LAG:
+                contraction_on_partitions(j - LAG, y_of[j - LAG])

@@ -100,11 +100,11 @@ def tile_digitcaps_t_v_kernel(tc, x, W, s, grad_out, out):
             nc.vector.scalar_tensor_tensor(
                 out=c1[:], in0=tau[:], scalar=2.0, in1=c0[:], op0=ALU.subtract, op1=ALU.mult
             )
-            r = work.tile([P, GROUP * N], F32)
-            nc.scalar.activation(out=r[:], in_=c1[:], func=ACT.Square)
+            sc = work.tile([P, GROUP * N], F32)
+            nc.vector.tensor_tensor(out=sc[:], in0=s_flat, in1=c1[:], op=ALU.mult)
             y = ahead.tile([P, GROUP, PACK, P], F32)
-            nc.gpsimd.tensor_tensor(
-                out=y[:].rearrange("p t u i -> p (t u i)"), in0=s_flat, in1=r[:], op=ALU.mult
+            nc.vector.tensor_tensor(
+                out=y[:].rearrange("p t u i -> p (t u i)"), in0=sc[:], in1=c1[:], op=ALU.mult
             )
             return y
 
@@ -158,12 +158,9 @@ def tile_digitcaps_t_v_kernel(tc, x, W, s, grad_out, out):
                         start=True,
                         stop=True,
                     )
-                    if j >= GROUPS // 2 and h == HALVES - 1:
-                        nc.scalar.activation(
-                            out=o_sb[:, cols], in_=o_ps[:], func=ACT.Copy, scale=1.0 / P
-                        )
-                    else:
-                        nc.vector.tensor_scalar_mul(out=o_sb[:, cols], in0=o_ps[:], scalar1=1.0 / P)
+                    nc.scalar.activation(
+                        out=o_sb[:, cols], in_=o_ps[:], func=ACT.Copy, scale=1.0 / P
+                    )
                 nc.sync.dma_start(out=out_rows[:, j * GROUP + t, :], in_=o_sb[:])
 
         y_of = {}

@@ -4,6 +4,7 @@ from concourse.masks import make_identity
 F32 = mybir.dt.float32
 BF16 = mybir.dt.bfloat16
 U32 = mybir.dt.uint32
+I32 = mybir.dt.int32
 U8 = mybir.dt.uint8
 E4M3_X4 = mybir.dt.float8_e4m3fn_x4
 E5M2_X4 = mybir.dt.float8_e5m2_x4
@@ -73,8 +74,6 @@ def tile_digitcaps_t_v_kernel(tc, x, W, s, grad_out, out):
 
         ident_f32 = const.tile([P, P], F32)
         make_identity(nc, ident_f32[:])
-        ident_bf16 = const.tile([P, P], BF16)
-        make_identity(nc, ident_bf16[:])
         one = const.tile([P, 1], F32)
         nc.vector.memset(one[:], 1.0)
         warm = const.tile([P, 1], F32)
@@ -86,6 +85,23 @@ def tile_digitcaps_t_v_kernel(tc, x, W, s, grad_out, out):
 
         def rows_on_partitions(j):
             s_flat = s_sb[j][:].rearrange("p t n -> p (t n)")
+            s_abs = work.tile([P, GROUP * N], I32)
+            nc.vector.tensor_scalar(
+                out=s_abs[:],
+                in0=s_flat.bitcast(I32),
+                scalar1=0x7FFFFFFF,
+                scalar2=None,
+                op0=ALU.bitwise_and,
+            )
+            ag = ahead.tile([P, GROUP, PACK, P], F32)
+            nc.vector.scalar_tensor_tensor(
+                out=ag[:].rearrange("p t u i -> p (t u i)"),
+                in0=s_abs[:].bitcast(F32),
+                scalar=2.0,
+                in1=g_sb[j][:].rearrange("p t n -> p (t n)"),
+                op0=ALU.mult,
+                op1=ALU.mult,
+            )
             sq = work.tile([P, GROUP * N], F32)
             nc.scalar.activation(out=sq[:], in_=s_flat, func=ACT.Square)
             den = work.tile([P, GROUP * N], F32)
@@ -96,34 +112,32 @@ def tile_digitcaps_t_v_kernel(tc, x, W, s, grad_out, out):
             nc.vector.scalar_tensor_tensor(
                 out=tau[:], in0=sq[:], scalar=1.0, in1=c0[:], op0=ALU.add, op1=ALU.mult
             )
-            c1 = work.tile([P, GROUP * N], F32)
+            c1 = ahead.tile([P, GROUP, PACK, P], F32)
             nc.vector.scalar_tensor_tensor(
-                out=c1[:], in0=tau[:], scalar=2.0, in1=c0[:], op0=ALU.subtract, op1=ALU.mult
+                out=c1[:].rearrange("p t u i -> p (t u i)"),
+                in0=tau[:],
+                scalar=2.0,
+                in1=c0[:],
+                op0=ALU.subtract,
+                op1=ALU.mult,
             )
-            sc = work.tile([P, GROUP * N], F32)
-            nc.vector.tensor_tensor(out=sc[:], in0=s_flat, in1=c1[:], op=ALU.mult)
-            y = ahead.tile([P, GROUP, PACK, P], F32)
-            nc.vector.tensor_tensor(
-                out=y[:].rearrange("p t u i -> p (t u i)"), in0=sc[:], in1=c1[:], op=ALU.mult
-            )
-            return y
+            return c1, ag
 
-        def contraction_on_partitions(j, y):
-            g_ps = psum_t.tile([P, GROUP, PACK, P], BF16)
+        def contraction_on_partitions(j, c1, ag):
             f = work.tile([P, GROUP, P, PACK], F32)
+            ag_ps_of = []
             for t in range(GROUP):
-                y_ps = psum_t.tile([P, PACK, P], F32)
+                c_ps = psum_t.tile([P, PACK, P], F32)
                 for u in range(PACK):
-                    nc.tensor.transpose(y_ps[:, u, :], y[:, t, u, :], ident_f32[:])
+                    nc.tensor.transpose(c_ps[:, u, :], c1[:, t, u, :], ident_f32[:])
+                ag_ps = psum_t.tile([P, PACK, P], F32)
                 for u in range(PACK):
-                    nc.tensor.transpose(
-                        g_ps[:, t, u, :], g_sb[j][:, t, u * P : (u + 1) * P], ident_bf16[:]
-                    )
+                    nc.tensor.transpose(ag_ps[:, u, :], ag[:, t, u, :], ident_f32[:])
+                ag_ps_of.append(ag_ps)
                 nc.scalar.activation(
                     out=f[:, t, :, :],
-                    in_=y_ps[:].rearrange("i u b -> i b u"),
-                    func=ACT.Abs,
-                    scale=2.0,
+                    in_=c_ps[:].rearrange("i u b -> i b u"),
+                    func=ACT.Square,
                 )
             ds = work.tile([P, GROUP, P, PACK], BF16, align_bytes=64)
             for t in range(GROUP):
@@ -131,7 +145,7 @@ def tile_digitcaps_t_v_kernel(tc, x, W, s, grad_out, out):
                     out=ds[:, t, :, :],
                     in0=f[:, t, :, :],
                     scalar=0.0,
-                    in1=g_ps[:, t, :, :].rearrange("i u b -> i b u"),
+                    in1=ag_ps_of[t][:].rearrange("i u b -> i b u"),
                     op0=ALU.max,
                     op1=ALU.mult,
                 )
@@ -168,4 +182,4 @@ def tile_digitcaps_t_v_kernel(tc, x, W, s, grad_out, out):
             if j < GROUPS:
                 y_of[j] = rows_on_partitions(j)
             if j >= LAG:
-                contraction_on_partitions(j - LAG, y_of[j - LAG])
+                contraction_on_partitions(j - LAG, y_of[j - LAG][0], y_of[j - LAG][1])

@@ -157,6 +157,9 @@ def tile_digitcaps_t_v_kernel(tc, x, W, s, grad_out, out):
                 scales=ds_scales[:],
                 in_=ds[:].rearrange("i t b u -> i (t b u)"),
             )
+            return ds_codes, ds_scales
+
+        def products(j, ds_codes, ds_scales):
             for t in range(GROUP):
                 rows = slice(t * P, (t + 1) * P)
                 o_sb = work.tile([P, K], F32)
@@ -172,14 +175,30 @@ def tile_digitcaps_t_v_kernel(tc, x, W, s, grad_out, out):
                         start=True,
                         stop=True,
                     )
-                    nc.scalar.activation(
-                        out=o_sb[:, cols], in_=o_ps[:], func=ACT.Copy, scale=1.0 / P
-                    )
+                    if (j == GROUPS - 1 and h == HALVES - 1) or (
+                        j >= 3 and t == GROUP - 1 and h == HALVES - 1
+                    ):
+                        nc.vector.tensor_scalar(
+                            out=o_sb[:, cols],
+                            in0=o_ps[:],
+                            scalar1=1.0 / P,
+                            scalar2=None,
+                            op0=ALU.mult,
+                        )
+                    else:
+                        nc.scalar.activation(
+                            out=o_sb[:, cols], in_=o_ps[:], func=ACT.Copy, scale=1.0 / P
+                        )
                 nc.sync.dma_start(out=out_rows[:, j * GROUP + t, :], in_=o_sb[:])
 
         y_of = {}
+        q_of = {}
         for j in range(GROUPS + LAG):
             if j < GROUPS:
                 y_of[j] = rows_on_partitions(j)
+            if 0 <= j - LAG + 1 < GROUPS:
+                q_of[j - LAG + 1] = contraction_on_partitions(
+                    j - LAG + 1, y_of[j - LAG + 1][0], y_of[j - LAG + 1][1]
+                )
             if j >= LAG:
-                contraction_on_partitions(j - LAG, y_of[j - LAG][0], y_of[j - LAG][1])
+                products(j - LAG, q_of[j - LAG][0], q_of[j - LAG][1])

@@ -18,11 +18,9 @@ N = 512
 K = 1024
 E_PAIRS = 4
 BLOCKS = ROWS // P
-GROUP = 2
-GROUPS = BLOCKS // GROUP
+SIZES = (1, 1, 2, 2, 2, 2, 2, 2, 1, 1)
 BANK = 512
 HALVES = K // BANK
-LAG = 2
 
 FLOPS = 2 * ROWS * K * N
 BYTES = 2 * K * N + 4 * ROWS * N + 2 * ROWS * N + 4 * ROWS * K
@@ -50,6 +48,9 @@ def quantise_w(nc, const, psum, w_sb, ident_f32, w_codes, w_scales):
 
 def tile_digitcaps_t_v_kernel(tc, x, W, s, grad_out, out):
     nc = tc.nc
+    assert sum(SIZES) == BLOCKS
+    groups = len(SIZES)
+    first_block = [sum(SIZES[:g]) for g in range(groups)]
     s_rows = s.rearrange("(p t) c d -> p t (c d)", t=BLOCKS)
     g_rows = grad_out.rearrange("(p t) c d o -> p t (c d o)", t=BLOCKS)
     out_rows = out.rearrange("(p t) q e -> p t (q e)", t=BLOCKS)
@@ -58,19 +59,19 @@ def tile_digitcaps_t_v_kernel(tc, x, W, s, grad_out, out):
     with (
         tc.tile_pool(name="const", bufs=1) as const,
         tc.tile_pool(name="work", bufs=3) as work,
-        tc.tile_pool(name="ahead", bufs=LAG + 2) as ahead,
+        tc.tile_pool(name="ahead", bufs=4) as ahead,
         tc.psum_pool(name="psum_t", bufs=2) as psum_t,
         tc.psum_pool(name="psum_o", bufs=4) as psum_o,
     ):
-        s_sb = [const.tile([P, GROUP, N], F32, name="s_sb%d" % j) for j in range(GROUPS)]
-        g_sb = [const.tile([P, GROUP, N], BF16, name="g_sb%d" % j) for j in range(GROUPS)]
+        s_sb = [const.tile([P, SIZES[g], N], F32, name="s_sb%d" % g) for g in range(groups)]
+        g_sb = [const.tile([P, SIZES[g], N], BF16, name="g_sb%d" % g) for g in range(groups)]
         w_sb = const.tile([P, N * 8], BF16)
-        for j in range(GROUPS):
-            blocks = slice(j * GROUP, (j + 1) * GROUP)
-            nc.sync.dma_start(out=s_sb[j][:], in_=s_rows[:, blocks, :])
-            if j == 0:
+        for g in range(groups):
+            blocks = slice(first_block[g], first_block[g] + SIZES[g])
+            nc.sync.dma_start(out=s_sb[g][:], in_=s_rows[:, blocks, :])
+            if g == 0:
                 nc.sync.dma_start(out=w_sb[:], in_=w_rows)
-            nc.sync.dma_start(out=g_sb[j][:], in_=g_rows[:, blocks, :])
+            nc.sync.dma_start(out=g_sb[g][:], in_=g_rows[:, blocks, :])
 
         ident_f32 = const.tile([P, P], F32)
         make_identity(nc, ident_f32[:])
@@ -83,9 +84,10 @@ def tile_digitcaps_t_v_kernel(tc, x, W, s, grad_out, out):
         w_scales = const.tile([P, K], U8, align_bytes=64)
         quantise_w(nc, const, psum_o, w_sb, ident_f32, w_codes, w_scales)
 
-        def rows_on_partitions(j):
-            s_flat = s_sb[j][:].rearrange("p t n -> p (t n)")
-            s_abs = work.tile([P, GROUP * N], I32)
+        def rows_on_partitions(g):
+            width = SIZES[g] * N
+            s_flat = s_sb[g][:].rearrange("p t n -> p (t n)")
+            s_abs = work.tile([P, width], I32)
             nc.vector.tensor_scalar(
                 out=s_abs[:],
                 in0=s_flat.bitcast(I32),
@@ -93,26 +95,26 @@ def tile_digitcaps_t_v_kernel(tc, x, W, s, grad_out, out):
                 scalar2=None,
                 op0=ALU.bitwise_and,
             )
-            ag = ahead.tile([P, GROUP, PACK, P], F32)
+            ag = ahead.tile([P, SIZES[g], PACK, P], F32)
             nc.vector.scalar_tensor_tensor(
                 out=ag[:].rearrange("p t u i -> p (t u i)"),
                 in0=s_abs[:].bitcast(F32),
                 scalar=2.0,
-                in1=g_sb[j][:].rearrange("p t n -> p (t n)"),
+                in1=g_sb[g][:].rearrange("p t n -> p (t n)"),
                 op0=ALU.mult,
                 op1=ALU.mult,
             )
-            sq = work.tile([P, GROUP * N], F32)
+            sq = work.tile([P, width], F32)
             nc.scalar.activation(out=sq[:], in_=s_flat, func=ACT.Square)
-            den = work.tile([P, GROUP * N], F32)
+            den = work.tile([P, width], F32)
             nc.scalar.activation(out=den[:], in_=sq[:], func=ACT.Square, bias=one[:])
-            c0 = work.tile([P, GROUP * N], F32)
+            c0 = work.tile([P, width], F32)
             nc.scalar.activation(out=c0[:], in_=den[:], func=ACT.Abs_reciprocal_sqrt)
-            tau = work.tile([P, GROUP * N], F32)
+            tau = work.tile([P, width], F32)
             nc.vector.scalar_tensor_tensor(
                 out=tau[:], in0=sq[:], scalar=1.0, in1=c0[:], op0=ALU.add, op1=ALU.mult
             )
-            c1 = ahead.tile([P, GROUP, PACK, P], F32)
+            c1 = ahead.tile([P, SIZES[g], PACK, P], F32)
             nc.vector.scalar_tensor_tensor(
                 out=c1[:].rearrange("p t u i -> p (t u i)"),
                 in0=tau[:],
@@ -123,10 +125,10 @@ def tile_digitcaps_t_v_kernel(tc, x, W, s, grad_out, out):
             )
             return c1, ag
 
-        def contraction_on_partitions(j, c1, ag):
-            f = work.tile([P, GROUP, P, PACK], F32)
+        def contraction_on_partitions(g, c1, ag):
+            csq = work.tile([P, SIZES[g], P, PACK], F32)
             ag_ps_of = []
-            for t in range(GROUP):
+            for t in range(SIZES[g]):
                 c_ps = psum_t.tile([P, PACK, P], F32)
                 for u in range(PACK):
                     nc.tensor.transpose(c_ps[:, u, :], c1[:, t, u, :], ident_f32[:])
@@ -135,23 +137,22 @@ def tile_digitcaps_t_v_kernel(tc, x, W, s, grad_out, out):
                     nc.tensor.transpose(ag_ps[:, u, :], ag[:, t, u, :], ident_f32[:])
                 ag_ps_of.append(ag_ps)
                 nc.scalar.activation(
-                    out=f[:, t, :, :],
+                    out=csq[:, t, :, :],
                     in_=c_ps[:].rearrange("i u b -> i b u"),
                     func=ACT.Square,
                 )
-            ds = work.tile([P, GROUP, P, PACK], BF16, align_bytes=64)
-            for t in range(GROUP):
+            ds = work.tile([P, SIZES[g], P, PACK], BF16, align_bytes=64)
+            for t in range(SIZES[g]):
                 nc.vector.scalar_tensor_tensor(
                     out=ds[:, t, :, :],
-                    in0=f[:, t, :, :],
+                    in0=csq[:, t, :, :],
                     scalar=0.0,
                     in1=ag_ps_of[t][:].rearrange("i u b -> i b u"),
                     op0=ALU.max,
                     op1=ALU.mult,
                 )
-
-            ds_codes = work.tile([P, GROUP * P], U32, align_bytes=64)
-            ds_scales = work.tile([P, GROUP * P], U8, align_bytes=64)
+            ds_codes = work.tile([P, SIZES[g] * P], U32, align_bytes=64)
+            ds_scales = work.tile([P, SIZES[g] * P], U8, align_bytes=64)
             nc.vector.quantize_mx(
                 out=ds_codes[:].bitcast(E5M2_X4),
                 scales=ds_scales[:],
@@ -159,8 +160,8 @@ def tile_digitcaps_t_v_kernel(tc, x, W, s, grad_out, out):
             )
             return ds_codes, ds_scales
 
-        def products(j, ds_codes, ds_scales):
-            for t in range(GROUP):
+        def products(g, ds_codes, ds_scales):
+            for t in range(SIZES[g]):
                 rows = slice(t * P, (t + 1) * P)
                 o_sb = work.tile([P, K], F32)
                 for h in range(HALVES):
@@ -175,9 +176,7 @@ def tile_digitcaps_t_v_kernel(tc, x, W, s, grad_out, out):
                         start=True,
                         stop=True,
                     )
-                    if (j == GROUPS - 1 and h == HALVES - 1) or (
-                        j >= 3 and t == GROUP - 1 and h == HALVES - 1
-                    ):
+                    if (g == len(SIZES) - 1 and h == HALVES - 1) or (first_block[g] >= 6 and t == SIZES[g] - 1 and h == HALVES - 1):
                         nc.vector.tensor_scalar(
                             out=o_sb[:, cols],
                             in0=o_ps[:],
@@ -189,16 +188,16 @@ def tile_digitcaps_t_v_kernel(tc, x, W, s, grad_out, out):
                         nc.scalar.activation(
                             out=o_sb[:, cols], in_=o_ps[:], func=ACT.Copy, scale=1.0 / P
                         )
-                nc.sync.dma_start(out=out_rows[:, j * GROUP + t, :], in_=o_sb[:])
+                nc.sync.dma_start(out=out_rows[:, first_block[g] + t, :], in_=o_sb[:])
 
-        y_of = {}
-        q_of = {}
-        for j in range(GROUPS + LAG):
-            if j < GROUPS:
-                y_of[j] = rows_on_partitions(j)
-            if 0 <= j - LAG + 1 < GROUPS:
-                q_of[j - LAG + 1] = contraction_on_partitions(
-                    j - LAG + 1, y_of[j - LAG + 1][0], y_of[j - LAG + 1][1]
+        made = {}
+        quantised = {}
+        for step in range(groups + 2):
+            if step < groups:
+                made[step] = rows_on_partitions(step)
+            if 0 <= step - 1 < groups:
+                quantised[step - 1] = contraction_on_partitions(
+                    step - 1, made[step - 1][0], made[step - 1][1]
                 )
-            if j >= LAG:
-                products(j - LAG, q_of[j - LAG][0], q_of[j - LAG][1])
+            if step >= 2:
+                products(step - 2, quantised[step - 2][0], quantised[step - 2][1])

@@ -58,83 +58,87 @@ def tile_digitcaps_t_v_kernel(tc, x, W, s, grad_out, out):
 
     with (
         tc.tile_pool(name="const", bufs=1) as const,
-        tc.tile_pool(name="work", bufs=3) as work,
+        tc.tile_pool(name="work", bufs=4) as work,
         tc.tile_pool(name="ahead", bufs=4) as ahead,
+        tc.tile_pool(name="outs", bufs=4) as outs,
         tc.psum_pool(name="psum_t", bufs=2) as psum_t,
         tc.psum_pool(name="psum_o", bufs=4) as psum_o,
+        tc.manual_schedule(engines={mybir.EngineType.Activation}),
     ):
         s_sb = [const.tile([P, SIZES[g], N], F32, name="s_sb%d" % g) for g in range(groups)]
         g_sb = [const.tile([P, SIZES[g], N], BF16, name="g_sb%d" % g) for g in range(groups)]
+        a_sb = [const.tile([P, SIZES[g], N], I32, name="a_sb%d" % g) for g in range(groups)]
+        ag_sb = [const.tile([P, SIZES[g], PACK, P], F32, name="ag_sb%d" % g) for g in range(groups)]
         w_sb = const.tile([P, N * 8], BF16)
-        for g in range(groups):
+
+        def load(tiles, rows, g):
             blocks = slice(first_block[g], first_block[g] + SIZES[g])
-            nc.sync.dma_start(out=s_sb[g][:], in_=s_rows[:, blocks, :])
-            if g == 0:
-                nc.sync.dma_start(out=w_sb[:], in_=w_rows)
-            nc.sync.dma_start(out=g_sb[g][:], in_=g_rows[:, blocks, :])
+            nc.sync.dma_start(out=tiles[g][:], in_=rows[:, blocks, :])
+
+        load(s_sb, s_rows, 0)
+        load(s_sb, s_rows, 1)
+        nc.sync.dma_start(out=w_sb[:], in_=w_rows)
+        for g in range(2, groups):
+            load(s_sb, s_rows, g)
+        for g in range(groups):
+            load(g_sb, g_rows, g)
 
         ident_f32 = const.tile([P, P], F32)
         make_identity(nc, ident_f32[:])
         one = const.tile([P, 1], F32)
         nc.vector.memset(one[:], 1.0)
         warm = const.tile([P, 1], F32)
-        nc.scalar.activation(out=warm[:], in_=one[:], func=ACT.Abs_reciprocal_sqrt)
+        nc.scalar.activation(out=warm[:], in_=one[:], func=ACT.Ln)
 
         w_codes = const.tile([P, K], U32, align_bytes=64)
         w_scales = const.tile([P, K], U8, align_bytes=64)
-        quantise_w(nc, const, psum_o, w_sb, ident_f32, w_codes, w_scales)
 
-        def rows_on_partitions(g):
-            width = SIZES[g] * N
-            s_flat = s_sb[g][:].rearrange("p t n -> p (t n)")
-            s_abs = work.tile([P, width], I32)
+        def magnitude(g):
             nc.vector.tensor_scalar(
-                out=s_abs[:],
-                in0=s_flat.bitcast(I32),
+                out=a_sb[g][:].rearrange("p t n -> p (t n)"),
+                in0=s_sb[g][:].rearrange("p t n -> p (t n)").bitcast(I32),
                 scalar1=0x7FFFFFFF,
                 scalar2=None,
                 op0=ALU.bitwise_and,
             )
-            ag = ahead.tile([P, SIZES[g], PACK, P], F32)
-            nc.vector.scalar_tensor_tensor(
-                out=ag[:].rearrange("p t u i -> p (t u i)"),
-                in0=s_abs[:].bitcast(F32),
-                scalar=2.0,
-                in1=g_sb[g][:].rearrange("p t n -> p (t n)"),
-                op0=ALU.mult,
-                op1=ALU.mult,
-            )
-            sq = work.tile([P, width], F32)
-            nc.scalar.activation(out=sq[:], in_=s_flat, func=ACT.Square)
-            den = work.tile([P, width], F32)
-            nc.scalar.activation(out=den[:], in_=sq[:], func=ACT.Square, bias=one[:])
-            c0 = work.tile([P, width], F32)
-            nc.scalar.activation(out=c0[:], in_=den[:], func=ACT.Abs_reciprocal_sqrt)
-            tau = work.tile([P, width], F32)
-            nc.vector.scalar_tensor_tensor(
-                out=tau[:], in0=sq[:], scalar=1.0, in1=c0[:], op0=ALU.add, op1=ALU.mult
-            )
-            c1 = ahead.tile([P, SIZES[g], PACK, P], F32)
-            nc.vector.scalar_tensor_tensor(
-                out=c1[:].rearrange("p t u i -> p (t u i)"),
-                in0=tau[:],
-                scalar=2.0,
-                in1=c0[:],
-                op0=ALU.subtract,
-                op1=ALU.mult,
-            )
-            return c1, ag
 
-        def contraction_on_partitions(g, c1, ag):
+        def logarithm(g):
+            nc.scalar.activation(
+                out=s_sb[g][:].rearrange("p t n -> p (t n)"),
+                in_=a_sb[g][:].rearrange("p t n -> p (t n)").bitcast(F32),
+                func=ACT.Ln,
+            )
+
+        def times_grad(g):
+            nc.vector.scalar_tensor_tensor(
+                out=ag_sb[g][:].rearrange("p t u i -> p (t u i)"),
+                in0=a_sb[g][:].rearrange("p t n -> p (t n)").bitcast(F32),
+                scalar=2.0**40,
+                in1=g_sb[g][:].rearrange("p t n -> p (t n)"),
+                op0=ALU.min,
+                op1=ALU.mult,
+            )
+
+        def sigmoid(g):
+            c = ahead.tile([P, SIZES[g], PACK, P], F32)
+            nc.scalar.activation(
+                out=c[:].rearrange("p t u i -> p (t u i)"),
+                in_=s_sb[g][:].rearrange("p t n -> p (t n)"),
+                func=ACT.Sigmoid,
+                scale=-2.0,
+            )
+            return c
+
+        def turn(g, c):
             csq = work.tile([P, SIZES[g], P, PACK], F32)
             ag_ps_of = []
             for t in range(SIZES[g]):
                 c_ps = psum_t.tile([P, PACK, P], F32)
                 for u in range(PACK):
-                    nc.tensor.transpose(c_ps[:, u, :], c1[:, t, u, :], ident_f32[:])
+                    nc.tensor.transpose(c_ps[:, u, :], c[:, t, u, :], ident_f32[:])
                 ag_ps = psum_t.tile([P, PACK, P], F32)
                 for u in range(PACK):
-                    nc.tensor.transpose(ag_ps[:, u, :], ag[:, t, u, :], ident_f32[:])
+                    nc.tensor.transpose(ag_ps[:, u, :], ag_sb[g][:, t, u, :], ident_f32[:])
                 ag_ps_of.append(ag_ps)
                 nc.scalar.activation(
                     out=csq[:, t, :, :],
@@ -146,9 +150,9 @@ def tile_digitcaps_t_v_kernel(tc, x, W, s, grad_out, out):
                 nc.vector.scalar_tensor_tensor(
                     out=ds[:, t, :, :],
                     in0=csq[:, t, :, :],
-                    scalar=0.0,
+                    scalar=2.0,
                     in1=ag_ps_of[t][:].rearrange("i u b -> i b u"),
-                    op0=ALU.max,
+                    op0=ALU.mult,
                     op1=ALU.mult,
                 )
             ds_codes = work.tile([P, SIZES[g] * P], U32, align_bytes=64)
@@ -163,7 +167,7 @@ def tile_digitcaps_t_v_kernel(tc, x, W, s, grad_out, out):
         def products(g, ds_codes, ds_scales):
             for t in range(SIZES[g]):
                 rows = slice(t * P, (t + 1) * P)
-                o_sb = work.tile([P, K], F32)
+                o_sb = outs.tile([P, K], F32)
                 for h in range(HALVES):
                     cols = slice(h * BANK, (h + 1) * BANK)
                     o_ps = psum_o.tile([P, BANK], F32)
@@ -176,7 +180,7 @@ def tile_digitcaps_t_v_kernel(tc, x, W, s, grad_out, out):
                         start=True,
                         stop=True,
                     )
-                    if (g == len(SIZES) - 1 and h == HALVES - 1) or (first_block[g] >= 6 and t == SIZES[g] - 1 and h == HALVES - 1):
+                    if h == HALVES - 1:
                         nc.vector.tensor_scalar(
                             out=o_sb[:, cols],
                             in0=o_ps[:],
@@ -190,14 +194,19 @@ def tile_digitcaps_t_v_kernel(tc, x, W, s, grad_out, out):
                         )
                 nc.sync.dma_start(out=out_rows[:, first_block[g] + t, :], in_=o_sb[:])
 
-        made = {}
-        quantised = {}
-        for step in range(groups + 2):
+        for g in range(groups):
+            magnitude(g)
+            logarithm(g)
+            if g == 1:
+                quantise_w(nc, const, psum_o, w_sb, ident_f32, w_codes, w_scales)
+
+        c_of = {}
+        codes = {}
+        for step in range(groups + 3):
             if step < groups:
-                made[step] = rows_on_partitions(step)
+                times_grad(step)
+                c_of[step] = sigmoid(step)
             if 0 <= step - 1 < groups:
-                quantised[step - 1] = contraction_on_partitions(
-                    step - 1, made[step - 1][0], made[step - 1][1]
-                )
-            if step >= 2:
-                products(step - 2, quantised[step - 2][0], quantised[step - 2][1])
+                codes[step - 1] = turn(step - 1, c_of[step - 1])
+            if step >= 3:
+                products(step - 3, codes[step - 3][0], codes[step - 3][1])

@@ -192,21 +192,21 @@ def tile_digitcaps_t_v_kernel(tc, x, W, s, grad_out, out):
                         nc.scalar.activation(
                             out=o_sb[:, cols], in_=o_ps[:], func=ACT.Copy, scale=1.0 / P
                         )
-                nc.sync.dma_start(out=out_rows[:, first_block[g] + t, :], in_=o_sb[:])
+                    nc.sync.dma_start(out=out_rows[:, first_block[g] + t, cols], in_=o_sb[:, cols])
 
         for g in range(groups):
             magnitude(g)
             logarithm(g)
-            if g == 1:
+            if g == groups - 1:
                 quantise_w(nc, const, psum_o, w_sb, ident_f32, w_codes, w_scales)
 
         c_of = {}
         codes = {}
-        for step in range(groups + 3):
+        for step in range(groups + 2):
             if step < groups:
                 times_grad(step)
                 c_of[step] = sigmoid(step)
             if 0 <= step - 1 < groups:
                 codes[step - 1] = turn(step - 1, c_of[step - 1])
-            if step >= 3:
-                products(step - 3, codes[step - 3][0], codes[step - 3][1])
+            if step >= 2:
+                products(step - 2, codes[step - 2][0], codes[step - 2][1])

@@ -58,7 +58,7 @@ def tile_digitcaps_t_v_kernel(tc, x, W, s, grad_out, out):
 
     with (
         tc.tile_pool(name="const", bufs=1) as const,
-        tc.tile_pool(name="work", bufs=4) as work,
+        tc.tile_pool(name="work", bufs=6) as work,
         tc.tile_pool(name="ahead", bufs=4) as ahead,
         tc.tile_pool(name="outs", bufs=4) as outs,
         tc.psum_pool(name="psum_t", bufs=2) as psum_t,
@@ -129,84 +129,77 @@ def tile_digitcaps_t_v_kernel(tc, x, W, s, grad_out, out):
             )
             return c
 
-        def turn(g, c):
-            csq = work.tile([P, SIZES[g], P, PACK], F32)
-            ag_ps_of = []
-            for t in range(SIZES[g]):
-                c_ps = psum_t.tile([P, PACK, P], F32)
-                for u in range(PACK):
-                    nc.tensor.transpose(c_ps[:, u, :], c[:, t, u, :], ident_f32[:])
-                ag_ps = psum_t.tile([P, PACK, P], F32)
-                for u in range(PACK):
-                    nc.tensor.transpose(ag_ps[:, u, :], ag_sb[g][:, t, u, :], ident_f32[:])
-                ag_ps_of.append(ag_ps)
-                nc.scalar.activation(
-                    out=csq[:, t, :, :],
-                    in_=c_ps[:].rearrange("i u b -> i b u"),
-                    func=ACT.Square,
-                )
-            ds = work.tile([P, SIZES[g], P, PACK], BF16, align_bytes=64)
-            for t in range(SIZES[g]):
-                nc.vector.scalar_tensor_tensor(
-                    out=ds[:, t, :, :],
-                    in0=csq[:, t, :, :],
-                    scalar=2.0,
-                    in1=ag_ps_of[t][:].rearrange("i u b -> i b u"),
-                    op0=ALU.mult,
-                    op1=ALU.mult,
-                )
-            ds_codes = work.tile([P, SIZES[g] * P], U32, align_bytes=64)
-            ds_scales = work.tile([P, SIZES[g] * P], U8, align_bytes=64)
+        def turn(g, t, c):
+            c_ps = psum_t.tile([P, PACK, P], F32)
+            for u in range(PACK):
+                nc.tensor.transpose(c_ps[:, u, :], c[:, t, u, :], ident_f32[:])
+            ag_ps = psum_t.tile([P, PACK, P], F32)
+            for u in range(PACK):
+                nc.tensor.transpose(ag_ps[:, u, :], ag_sb[g][:, t, u, :], ident_f32[:])
+            csq = work.tile([P, P, PACK], F32)
+            nc.scalar.activation(
+                out=csq[:], in_=c_ps[:].rearrange("i u b -> i b u"), func=ACT.Square
+            )
+            ds = work.tile([P, P, PACK], BF16, align_bytes=64)
+            nc.vector.scalar_tensor_tensor(
+                out=ds[:],
+                in0=csq[:],
+                scalar=2.0,
+                in1=ag_ps[:].rearrange("i u b -> i b u"),
+                op0=ALU.mult,
+                op1=ALU.mult,
+            )
+            ds_codes = work.tile([P, P], U32, align_bytes=64)
+            ds_scales = work.tile([P, P], U8, align_bytes=64)
             nc.vector.quantize_mx(
                 out=ds_codes[:].bitcast(E5M2_X4),
                 scales=ds_scales[:],
-                in_=ds[:].rearrange("i t b u -> i (t b u)"),
+                in_=ds[:].rearrange("i b u -> i (b u)"),
             )
             return ds_codes, ds_scales
 
-        def products(g, ds_codes, ds_scales):
-            for t in range(SIZES[g]):
-                rows = slice(t * P, (t + 1) * P)
-                o_sb = outs.tile([P, K], F32)
-                for h in range(HALVES):
-                    cols = slice(h * BANK, (h + 1) * BANK)
-                    o_ps = psum_o.tile([P, BANK], F32)
-                    nc.tensor.matmul_mx(
-                        out=o_ps[:],
-                        lhsT=ds_codes[:, rows].bitcast(E5M2_X4),
-                        lhsT_scale=ds_scales[:, rows],
-                        rhs=w_codes[:, cols].bitcast(E4M3_X4),
-                        rhs_scale=w_scales[:, cols],
-                        start=True,
-                        stop=True,
+        def products(block, ds_codes, ds_scales):
+            o_sb = outs.tile([P, K], F32)
+            for h in range(HALVES):
+                cols = slice(h * BANK, (h + 1) * BANK)
+                o_ps = psum_o.tile([P, BANK], F32)
+                nc.tensor.matmul_mx(
+                    out=o_ps[:],
+                    lhsT=ds_codes[:].bitcast(E5M2_X4),
+                    lhsT_scale=ds_scales[:],
+                    rhs=w_codes[:, cols].bitcast(E4M3_X4),
+                    rhs_scale=w_scales[:, cols],
+                    start=True,
+                    stop=True,
+                )
+                if h == HALVES - 1:
+                    nc.vector.tensor_scalar(
+                        out=o_sb[:, cols],
+                        in0=o_ps[:],
+                        scalar1=1.0 / P,
+                        scalar2=None,
+                        op0=ALU.mult,
                     )
-                    if h == HALVES - 1:
-                        nc.vector.tensor_scalar(
-                            out=o_sb[:, cols],
-                            in0=o_ps[:],
-                            scalar1=1.0 / P,
-                            scalar2=None,
-                            op0=ALU.mult,
-                        )
-                    else:
-                        nc.scalar.activation(
-                            out=o_sb[:, cols], in_=o_ps[:], func=ACT.Copy, scale=1.0 / P
-                        )
-                    nc.sync.dma_start(out=out_rows[:, first_block[g] + t, cols], in_=o_sb[:, cols])
+                else:
+                    nc.scalar.activation(
+                        out=o_sb[:, cols], in_=o_ps[:], func=ACT.Copy, scale=1.0 / P
+                    )
+                nc.sync.dma_start(out=out_rows[:, block, cols], in_=o_sb[:, cols])
 
         for g in range(groups):
             magnitude(g)
             logarithm(g)
-            if g == groups - 1:
-                quantise_w(nc, const, psum_o, w_sb, ident_f32, w_codes, w_scales)
+        quantise_w(nc, const, psum_o, w_sb, ident_f32, w_codes, w_scales)
 
+        group_of = [g for g in range(groups) for t in range(SIZES[g])]
         c_of = {}
         codes = {}
-        for step in range(groups + 2):
-            if step < groups:
-                times_grad(step)
-                c_of[step] = sigmoid(step)
-            if 0 <= step - 1 < groups:
-                codes[step - 1] = turn(step - 1, c_of[step - 1])
-            if step >= 2:
-                products(step - 2, codes[step - 2][0], codes[step - 2][1])
+        for step in range(BLOCKS + 4):
+            if step < BLOCKS and step == first_block[group_of[step]]:
+                times_grad(group_of[step])
+                c_of[group_of[step]] = sigmoid(group_of[step])
+            if 0 <= step - 2 < BLOCKS:
+                g = group_of[step - 2]
+                codes[step - 2] = turn(g, step - 2 - first_block[g], c_of[g])
+            if step >= 4:
+                products(step - 4, codes[step - 4][0], codes[step - 4][1])

@@ -19,6 +19,7 @@ K = 1024
 E_PAIRS = 4
 BLOCKS = ROWS // P
 SIZES = (1, 1, 2, 2, 2, 2, 2, 2, 1, 1)
+AHEAD = 2
 BANK = 512
 HALVES = K // BANK
 
@@ -26,17 +27,18 @@ FLOPS = 2 * ROWS * K * N
 BYTES = 2 * K * N + 4 * ROWS * N + 2 * ROWS * N + 4 * ROWS * K
 
 
-def quantise_w(nc, const, psum, w_sb, ident_f32, w_codes, w_scales):
+def turn_w(nc, psum, w_sb, ident_f32, w_grouped, w):
     w_words = w_sb[:].bitcast(F32).rearrange("p (u i w) -> p u i w", u=PACK, i=P, w=E_PAIRS)
-    w_grouped = const.tile([P, P, E_PAIRS, 2, PACK], BF16, align_bytes=64)
-    for w in range(E_PAIRS):
-        w_ps = psum.tile([P, PACK, P], F32, tag="o_ps")
-        for u in range(PACK):
-            nc.tensor.transpose(w_ps[:, u, :], w_words[:, u, :, w], ident_f32[:])
-        nc.vector.tensor_copy(
-            out=w_grouped[:, :, w, :, :],
-            in_=w_ps[:].bitcast(BF16).rearrange("i u (p l) -> i p l u", l=2),
-        )
+    w_ps = psum.tile([P, PACK, P], F32, tag="o_ps")
+    for u in range(PACK):
+        nc.tensor.transpose(w_ps[:, u, :], w_words[:, u, :, w], ident_f32[:])
+    nc.vector.tensor_copy(
+        out=w_grouped[:, :, w, :, :],
+        in_=w_ps[:].bitcast(BF16).rearrange("i u (p l) -> i p l u", l=2),
+    )
+
+
+def quantise_w(nc, w_grouped, w_codes, w_scales):
     w_flat = w_grouped[:].rearrange("i p w l u -> i (p w l u)")
     for h in range(HALVES):
         nc.vector.quantize_mx(
@@ -63,7 +65,7 @@ def tile_digitcaps_t_v_kernel(tc, x, W, s, grad_out, out):
         tc.tile_pool(name="outs", bufs=4) as outs,
         tc.psum_pool(name="psum_t", bufs=2) as psum_t,
         tc.psum_pool(name="psum_o", bufs=4) as psum_o,
-        tc.manual_schedule(engines={mybir.EngineType.Activation}),
+        tc.manual_schedule(engines={mybir.EngineType.Activation, mybir.EngineType.DVE}),
     ):
         s_sb = [const.tile([P, SIZES[g], N], F32, name="s_sb%d" % g) for g in range(groups)]
         g_sb = [const.tile([P, SIZES[g], N], BF16, name="g_sb%d" % g) for g in range(groups)]
@@ -92,6 +94,7 @@ def tile_digitcaps_t_v_kernel(tc, x, W, s, grad_out, out):
 
         w_codes = const.tile([P, K], U32, align_bytes=64)
         w_scales = const.tile([P, K], U8, align_bytes=64)
+        w_grouped = const.tile([P, P, E_PAIRS, 2, PACK], BF16, align_bytes=64)
 
         def magnitude(g):
             nc.vector.tensor_scalar(
@@ -149,6 +152,9 @@ def tile_digitcaps_t_v_kernel(tc, x, W, s, grad_out, out):
                 op0=ALU.mult,
                 op1=ALU.mult,
             )
+            return ds
+
+        def quantise(ds):
             ds_codes = work.tile([P, P], U32, align_bytes=64)
             ds_scales = work.tile([P, P], U8, align_bytes=64)
             nc.vector.quantize_mx(
@@ -189,17 +195,25 @@ def tile_digitcaps_t_v_kernel(tc, x, W, s, grad_out, out):
         for g in range(groups):
             magnitude(g)
             logarithm(g)
-        quantise_w(nc, const, psum_o, w_sb, ident_f32, w_codes, w_scales)
+            if g % 2 == 1 and g // 2 < E_PAIRS:
+                turn_w(nc, psum_o, w_sb, ident_f32, w_grouped, g // 2)
+        quantise_w(nc, w_grouped, w_codes, w_scales)
+        for g in range(AHEAD):
+            times_grad(g)
 
         group_of = [g for g in range(groups) for t in range(SIZES[g])]
         c_of = {}
+        ds_of = {}
         codes = {}
         for step in range(BLOCKS + 4):
             if step < BLOCKS and step == first_block[group_of[step]]:
-                times_grad(group_of[step])
+                if group_of[step] + AHEAD < groups:
+                    times_grad(group_of[step] + AHEAD)
                 c_of[group_of[step]] = sigmoid(group_of[step])
             if 0 <= step - 2 < BLOCKS:
                 g = group_of[step - 2]
-                codes[step - 2] = turn(g, step - 2 - first_block[g], c_of[g])
+                ds_of[step - 2] = turn(g, step - 2 - first_block[g], c_of[g])
             if step >= 4:
                 products(step - 4, codes[step - 4][0], codes[step - 4][1])
+            if 0 <= step - 2 < BLOCKS:
+                codes[step - 2] = quantise(ds_of[step - 2])

@@ -19,7 +19,15 @@ K = 1024
 E_PAIRS = 4
 BLOCKS = ROWS // P
 SIZES = (1, 1, 2, 2, 2, 2, 2, 2, 1, 1)
+W_COLS = 4096
+LOADS = [("s", 0), ("s", 1), ("w", 0), ("s", 2), ("s", 3), ("s", 4), ("s", 5), ("s", 6), ("s", 7), ("s", 8), ("s", 9), ("g", 0), ("g", 1), ("g", 2), ("g", 3), ("g", 4), ("g", 5), ("g", 6), ("g", 7), ("g", 8), ("g", 9)]
+PHASE_1 = [("s", 0), ("s", 1), ("w", 0), ("s", 2), ("s", 3), ("w", 1), ("s", 4), ("s", 5), ("w", 2), ("s", 6), ("s", 7), ("w", 3), ("s", 8), ("s", 9), ("q", 0), ("g", 0), ("g", 1), ("g", 2), ("g", 3), ("g", 4)]
+S_BOTH = ()
+V_BOTH = (1, 3, 5, 7)
+V_GRADS = 5
+G_AHEAD = 2
 AHEAD = 2
+LAG = 4
 BANK = 512
 HALVES = K // BANK
 
@@ -62,6 +70,7 @@ def tile_digitcaps_t_v_kernel(tc, x, W, s, grad_out, out):
         tc.tile_pool(name="const", bufs=1) as const,
         tc.tile_pool(name="work", bufs=6) as work,
         tc.tile_pool(name="ahead", bufs=4) as ahead,
+        tc.tile_pool(name="turns", bufs=5) as turns,
         tc.tile_pool(name="outs", bufs=4) as outs,
         tc.psum_pool(name="psum_t", bufs=2) as psum_t,
         tc.psum_pool(name="psum_o", bufs=4) as psum_o,
@@ -70,20 +79,21 @@ def tile_digitcaps_t_v_kernel(tc, x, W, s, grad_out, out):
         s_sb = [const.tile([P, SIZES[g], N], F32, name="s_sb%d" % g) for g in range(groups)]
         g_sb = [const.tile([P, SIZES[g], N], BF16, name="g_sb%d" % g) for g in range(groups)]
         a_sb = [const.tile([P, SIZES[g], N], I32, name="a_sb%d" % g) for g in range(groups)]
-        ag_sb = [const.tile([P, SIZES[g], PACK, P], F32, name="ag_sb%d" % g) for g in range(groups)]
+        ag_sb = [const.tile([P, SIZES[g], PACK, P], F32, name="ag_sb%d" % g) for g in range(V_GRADS)]
         w_sb = const.tile([P, N * 8], BF16)
 
         def load(tiles, rows, g):
             blocks = slice(first_block[g], first_block[g] + SIZES[g])
             nc.sync.dma_start(out=tiles[g][:], in_=rows[:, blocks, :])
 
-        load(s_sb, s_rows, 0)
-        load(s_sb, s_rows, 1)
-        nc.sync.dma_start(out=w_sb[:], in_=w_rows)
-        for g in range(2, groups):
-            load(s_sb, s_rows, g)
-        for g in range(groups):
-            load(g_sb, g_rows, g)
+        for kind, g in LOADS:
+            if kind == "w":
+                cols = slice(g * W_COLS, (g + 1) * W_COLS)
+                nc.sync.dma_start(out=w_sb[:, cols], in_=w_rows[:, cols])
+            elif kind == "s":
+                load(s_sb, s_rows, g)
+            else:
+                load(g_sb, g_rows, g)
 
         ident_f32 = const.tile([P, P], F32)
         make_identity(nc, ident_f32[:])
@@ -92,6 +102,7 @@ def tile_digitcaps_t_v_kernel(tc, x, W, s, grad_out, out):
         warm = const.tile([P, 1], F32)
         nc.scalar.activation(out=warm[:], in_=one[:], func=ACT.Ln)
 
+        group_of = [g for g in range(groups) for t in range(SIZES[g])]
         w_codes = const.tile([P, K], U32, align_bytes=64)
         w_scales = const.tile([P, K], U8, align_bytes=64)
         w_grouped = const.tile([P, P, E_PAIRS, 2, PACK], BF16, align_bytes=64)
@@ -122,6 +133,24 @@ def tile_digitcaps_t_v_kernel(tc, x, W, s, grad_out, out):
                 op1=ALU.mult,
             )
 
+        ag_of = {}
+        for g in range(V_GRADS):
+            for t in range(SIZES[g]):
+                ag_of[first_block[g] + t] = ag_sb[g][:, t, :, :]
+
+        def times_grad_block(block):
+            g = group_of[block]
+            t = block - first_block[g]
+            ag = turns.tile([P, PACK, P], F32, tag="turn", align_bytes=64)
+            for c in range(0, N, 512):
+                nc.gpsimd.tensor_tensor(
+                    out=ag[:].rearrange("p u i -> p (u i)")[:, c : c + 512],
+                    in0=a_sb[g][:, t, c : c + 512].bitcast(F32),
+                    in1=g_sb[g][:, t, c : c + 512],
+                    op=ALU.mult,
+                )
+            ag_of[block] = ag[:]
+
         def sigmoid(g):
             c = ahead.tile([P, SIZES[g], PACK, P], F32)
             nc.scalar.activation(
@@ -138,12 +167,12 @@ def tile_digitcaps_t_v_kernel(tc, x, W, s, grad_out, out):
                 nc.tensor.transpose(c_ps[:, u, :], c[:, t, u, :], ident_f32[:])
             ag_ps = psum_t.tile([P, PACK, P], F32)
             for u in range(PACK):
-                nc.tensor.transpose(ag_ps[:, u, :], ag_sb[g][:, t, u, :], ident_f32[:])
+                nc.tensor.transpose(ag_ps[:, u, :], ag_of[first_block[g] + t][:, u, :], ident_f32[:])
             csq = work.tile([P, P, PACK], F32)
             nc.scalar.activation(
                 out=csq[:], in_=c_ps[:].rearrange("i u b -> i b u"), func=ACT.Square
             )
-            ds = work.tile([P, P, PACK], BF16, align_bytes=64)
+            ds = turns.tile([P, P, PACK], BF16, tag="turn", align_bytes=64)
             nc.vector.scalar_tensor_tensor(
                 out=ds[:],
                 in0=csq[:],
@@ -178,7 +207,7 @@ def tile_digitcaps_t_v_kernel(tc, x, W, s, grad_out, out):
                     start=True,
                     stop=True,
                 )
-                if h == HALVES - 1:
+                if (h == HALVES - 1 and block not in S_BOTH) or block in V_BOTH:
                     nc.vector.tensor_scalar(
                         out=o_sb[:, cols],
                         in0=o_ps[:],
@@ -192,28 +221,29 @@ def tile_digitcaps_t_v_kernel(tc, x, W, s, grad_out, out):
                     )
                 nc.sync.dma_start(out=out_rows[:, block, cols], in_=o_sb[:, cols])
 
-        for g in range(groups):
-            magnitude(g)
-            logarithm(g)
-            if g % 2 == 1 and g // 2 < E_PAIRS:
-                turn_w(nc, psum_o, w_sb, ident_f32, w_grouped, g // 2)
-        quantise_w(nc, w_grouped, w_codes, w_scales)
-        for g in range(AHEAD):
-            times_grad(g)
+        for kind, g in PHASE_1:
+            if kind == "s":
+                magnitude(g)
+                logarithm(g)
+            elif kind == "g":
+                times_grad(g)
+            elif kind == "w":
+                turn_w(nc, psum_o, w_sb, ident_f32, w_grouped, g)
+            else:
+                quantise_w(nc, w_grouped, w_codes, w_scales)
 
-        group_of = [g for g in range(groups) for t in range(SIZES[g])]
         c_of = {}
         ds_of = {}
         codes = {}
-        for step in range(BLOCKS + 4):
+        for step in range(BLOCKS + LAG):
             if step < BLOCKS and step == first_block[group_of[step]]:
-                if group_of[step] + AHEAD < groups:
-                    times_grad(group_of[step] + AHEAD)
                 c_of[group_of[step]] = sigmoid(group_of[step])
             if 0 <= step - 2 < BLOCKS:
                 g = group_of[step - 2]
                 ds_of[step - 2] = turn(g, step - 2 - first_block[g], c_of[g])
-            if step >= 4:
-                products(step - 4, codes[step - 4][0], codes[step - 4][1])
+            if step >= LAG:
+                products(step - LAG, codes[step - LAG][0], codes[step - LAG][1])
             if 0 <= step - 2 < BLOCKS:
                 codes[step - 2] = quantise(ds_of[step - 2])
+                if first_block[V_GRADS] <= step - 2 + G_AHEAD < BLOCKS:
+                    times_grad_block(step - 2 + G_AHEAD)

@@ -18,16 +18,21 @@ N = 512
 K = 1024
 E_PAIRS = 4
 BLOCKS = ROWS // P
-SIZES = (1, 1, 2, 2, 2, 2, 2, 2, 1, 1)
-W_COLS = 4096
-LOADS = [("s", 0), ("s", 1), ("w", 0), ("s", 2), ("s", 3), ("s", 4), ("s", 5), ("s", 6), ("s", 7), ("s", 8), ("s", 9), ("g", 0), ("g", 1), ("g", 2), ("g", 3), ("g", 4), ("g", 5), ("g", 6), ("g", 7), ("g", 8), ("g", 9)]
-PHASE_1 = [("s", 0), ("s", 1), ("w", 0), ("s", 2), ("s", 3), ("w", 1), ("s", 4), ("s", 5), ("w", 2), ("s", 6), ("s", 7), ("w", 3), ("s", 8), ("s", 9), ("q", 0), ("g", 0), ("g", 1), ("g", 2), ("g", 3), ("g", 4)]
+S_GROUPS = (1, 1, 2, 2, 2, 2, 2, 2, 1, 1)
+G_GROUPS = (1, 1, 2, 2, 2, 2, 2, 2, 1, 1)
+SIG_GROUPS = (1, 1, 2, 2, 2, 2, 2, 2, 1, 1)
+LOADS = [("s", 0), ("s", 1), ("s", 2), ("s", 3), ("s", 4), ("s", 5), ("s", 6), ("s", 7), ("s", 8), ("s", 9), ("g", 0), ("g", 1), ("w", 0), ("g", 2), ("g", 3), ("g", 4), ("g", 5), ("g", 6), ("g", 7), ("g", 8), ("g", 9)]
+PHASE_1 = [("s", 0), ("s", 1), ("s", 2), ("s", 3), ("s", 4), ("s", 5), ("s", 6), ("s", 7), ("s", 8), ("s", 9), ("g", 0), ("g", 1), ("h", 0), ("h", 1), ("x", 0), ("w", 1), ("x", 2), ("w", 3), ("q", 0)]
+V_BOTH = (1, 3)
 S_BOTH = ()
-V_BOTH = (1, 3, 5, 7)
-V_GRADS = 5
+FINE_STORES = 8
+V_GRADS = 2
 G_AHEAD = 2
-AHEAD = 2
-LAG = 4
+LEAD = 2
+DEPTH = 2
+LAG = 6
+QPAIR = False
+SQ_FIRST = False
 BANK = 512
 HALVES = K // BANK
 
@@ -35,15 +40,17 @@ FLOPS = 2 * ROWS * K * N
 BYTES = 2 * K * N + 4 * ROWS * N + 2 * ROWS * N + 4 * ROWS * K
 
 
-def turn_w(nc, psum, w_sb, ident_f32, w_grouped, w):
+def turn_w(nc, psum, w_sb, ident_f32, w_grouped, w, scalar):
     w_words = w_sb[:].bitcast(F32).rearrange("p (u i w) -> p u i w", u=PACK, i=P, w=E_PAIRS)
     w_ps = psum.tile([P, PACK, P], F32, tag="o_ps")
     for u in range(PACK):
         nc.tensor.transpose(w_ps[:, u, :], w_words[:, u, :, w], ident_f32[:])
-    nc.vector.tensor_copy(
-        out=w_grouped[:, :, w, :, :],
-        in_=w_ps[:].bitcast(BF16).rearrange("i u (p l) -> i p l u", l=2),
-    )
+    out = w_grouped[:, :, w, :, :]
+    in_ = w_ps[:].bitcast(BF16).rearrange("i u (p l) -> i p l u", l=2)
+    if scalar:
+        nc.scalar.copy(out=out, in_=in_)
+    else:
+        nc.vector.tensor_copy(out=out, in_=in_)
 
 
 def quantise_w(nc, w_grouped, w_codes, w_scales):
@@ -58,9 +65,10 @@ def quantise_w(nc, w_grouped, w_codes, w_scales):
 
 def tile_digitcaps_t_v_kernel(tc, x, W, s, grad_out, out):
     nc = tc.nc
-    assert sum(SIZES) == BLOCKS
-    groups = len(SIZES)
-    first_block = [sum(SIZES[:g]) for g in range(groups)]
+    assert sum(S_GROUPS) == sum(G_GROUPS) == sum(SIG_GROUPS) == BLOCKS
+    s_first = [sum(S_GROUPS[:g]) for g in range(len(S_GROUPS))]
+    g_first = [sum(G_GROUPS[:g]) for g in range(len(G_GROUPS))]
+    sig_first = [sum(SIG_GROUPS[:g]) for g in range(len(SIG_GROUPS))]
     s_rows = s.rearrange("(p t) c d -> p t (c d)", t=BLOCKS)
     g_rows = grad_out.rearrange("(p t) c d o -> p t (c d o)", t=BLOCKS)
     out_rows = out.rearrange("(p t) q e -> p t (q e)", t=BLOCKS)
@@ -70,30 +78,28 @@ def tile_digitcaps_t_v_kernel(tc, x, W, s, grad_out, out):
         tc.tile_pool(name="const", bufs=1) as const,
         tc.tile_pool(name="work", bufs=6) as work,
         tc.tile_pool(name="ahead", bufs=4) as ahead,
+        tc.tile_pool(name="squares", bufs=10) as squares,
         tc.tile_pool(name="turns", bufs=5) as turns,
         tc.tile_pool(name="outs", bufs=4) as outs,
         tc.psum_pool(name="psum_t", bufs=2) as psum_t,
         tc.psum_pool(name="psum_o", bufs=4) as psum_o,
         tc.manual_schedule(engines={mybir.EngineType.Activation, mybir.EngineType.DVE}),
     ):
-        s_sb = [const.tile([P, SIZES[g], N], F32, name="s_sb%d" % g) for g in range(groups)]
-        g_sb = [const.tile([P, SIZES[g], N], BF16, name="g_sb%d" % g) for g in range(groups)]
-        a_sb = [const.tile([P, SIZES[g], N], I32, name="a_sb%d" % g) for g in range(groups)]
-        ag_sb = [const.tile([P, SIZES[g], PACK, P], F32, name="ag_sb%d" % g) for g in range(V_GRADS)]
+        s_sb = const.tile([P, BLOCKS, N], F32)
+        a_sb = const.tile([P, BLOCKS, N], I32)
+        g_sb = const.tile([P, BLOCKS, N], BF16)
+        ag_sb = const.tile([P, max(V_GRADS, 1), PACK, P], F32)
         w_sb = const.tile([P, N * 8], BF16)
-
-        def load(tiles, rows, g):
-            blocks = slice(first_block[g], first_block[g] + SIZES[g])
-            nc.sync.dma_start(out=tiles[g][:], in_=rows[:, blocks, :])
 
         for kind, g in LOADS:
             if kind == "w":
-                cols = slice(g * W_COLS, (g + 1) * W_COLS)
-                nc.sync.dma_start(out=w_sb[:, cols], in_=w_rows[:, cols])
+                nc.sync.dma_start(out=w_sb[:], in_=w_rows)
             elif kind == "s":
-                load(s_sb, s_rows, g)
+                blocks = slice(s_first[g], s_first[g] + S_GROUPS[g])
+                nc.sync.dma_start(out=s_sb[:, blocks, :], in_=s_rows[:, blocks, :])
             else:
-                load(g_sb, g_rows, g)
+                blocks = slice(g_first[g], g_first[g] + G_GROUPS[g])
+                nc.sync.dma_start(out=g_sb[:, blocks, :], in_=g_rows[:, blocks, :])
 
         ident_f32 = const.tile([P, P], F32)
         make_identity(nc, ident_f32[:])
@@ -102,96 +108,90 @@ def tile_digitcaps_t_v_kernel(tc, x, W, s, grad_out, out):
         warm = const.tile([P, 1], F32)
         nc.scalar.activation(out=warm[:], in_=one[:], func=ACT.Ln)
 
-        group_of = [g for g in range(groups) for t in range(SIZES[g])]
         w_codes = const.tile([P, K], U32, align_bytes=64)
         w_scales = const.tile([P, K], U8, align_bytes=64)
         w_grouped = const.tile([P, P, E_PAIRS, 2, PACK], BF16, align_bytes=64)
 
-        def magnitude(g):
+        def magnitude(first, size):
+            blocks = slice(first, first + size)
             nc.vector.tensor_scalar(
-                out=a_sb[g][:].rearrange("p t n -> p (t n)"),
-                in0=s_sb[g][:].rearrange("p t n -> p (t n)").bitcast(I32),
+                out=a_sb[:, blocks, :].rearrange("p t n -> p (t n)"),
+                in0=s_sb[:, blocks, :].rearrange("p t n -> p (t n)").bitcast(I32),
                 scalar1=0x7FFFFFFF,
                 scalar2=None,
                 op0=ALU.bitwise_and,
             )
 
-        def logarithm(g):
+        def logarithm(first, size):
+            blocks = slice(first, first + size)
             nc.scalar.activation(
-                out=s_sb[g][:].rearrange("p t n -> p (t n)"),
-                in_=a_sb[g][:].rearrange("p t n -> p (t n)").bitcast(F32),
+                out=s_sb[:, blocks, :].rearrange("p t n -> p (t n)"),
+                in_=a_sb[:, blocks, :].rearrange("p t n -> p (t n)").bitcast(F32),
                 func=ACT.Ln,
             )
 
-        def times_grad(g):
+        def times_grad(first, size):
+            blocks = slice(first, first + size)
             nc.vector.scalar_tensor_tensor(
-                out=ag_sb[g][:].rearrange("p t u i -> p (t u i)"),
-                in0=a_sb[g][:].rearrange("p t n -> p (t n)").bitcast(F32),
+                out=ag_sb[:, blocks, :, :].rearrange("p t u i -> p (t u i)"),
+                in0=a_sb[:, blocks, :].rearrange("p t n -> p (t n)").bitcast(F32),
                 scalar=2.0**40,
-                in1=g_sb[g][:].rearrange("p t n -> p (t n)"),
+                in1=g_sb[:, blocks, :].rearrange("p t n -> p (t n)"),
                 op0=ALU.min,
                 op1=ALU.mult,
             )
 
         ag_of = {}
-        for g in range(V_GRADS):
-            for t in range(SIZES[g]):
-                ag_of[first_block[g] + t] = ag_sb[g][:, t, :, :]
+        for block in range(V_GRADS):
+            ag_of[block] = ag_sb[:, block, :, :]
 
         def times_grad_block(block):
-            g = group_of[block]
-            t = block - first_block[g]
             ag = turns.tile([P, PACK, P], F32, tag="turn", align_bytes=64)
-            for c in range(0, N, 512):
-                nc.gpsimd.tensor_tensor(
-                    out=ag[:].rearrange("p u i -> p (u i)")[:, c : c + 512],
-                    in0=a_sb[g][:, t, c : c + 512].bitcast(F32),
-                    in1=g_sb[g][:, t, c : c + 512],
-                    op=ALU.mult,
-                )
+            nc.gpsimd.tensor_tensor(
+                out=ag[:].rearrange("p u i -> p (u i)"),
+                in0=a_sb[:, block, :].bitcast(F32),
+                in1=g_sb[:, block, :],
+                op=ALU.mult,
+            )
             ag_of[block] = ag[:]
 
-        def sigmoid(g):
-            c = ahead.tile([P, SIZES[g], PACK, P], F32)
+        c_of = {}
+        csq_of = {}
+
+        def sigmoid(first, size):
+            blocks = slice(first, first + size)
+            c = ahead.tile([P, size, PACK, P], F32)
             nc.scalar.activation(
                 out=c[:].rearrange("p t u i -> p (t u i)"),
-                in_=s_sb[g][:].rearrange("p t n -> p (t n)"),
+                in_=s_sb[:, blocks, :].rearrange("p t n -> p (t n)"),
                 func=ACT.Sigmoid,
                 scale=-2.0,
             )
-            return c
+            for t in range(size):
+                c_of[first + t] = c[:, t, :, :]
 
-        def turn(g, t, c):
+        def square(block):
             c_ps = psum_t.tile([P, PACK, P], F32)
             for u in range(PACK):
-                nc.tensor.transpose(c_ps[:, u, :], c[:, t, u, :], ident_f32[:])
-            ag_ps = psum_t.tile([P, PACK, P], F32)
-            for u in range(PACK):
-                nc.tensor.transpose(ag_ps[:, u, :], ag_of[first_block[g] + t][:, u, :], ident_f32[:])
-            csq = work.tile([P, P, PACK], F32)
+                nc.tensor.transpose(c_ps[:, u, :], c_of[block][:, u, :], ident_f32[:])
+            csq = squares.tile([P, P, PACK], F32)
             nc.scalar.activation(
                 out=csq[:], in_=c_ps[:].rearrange("i u b -> i b u"), func=ACT.Square
             )
-            ds = turns.tile([P, P, PACK], BF16, tag="turn", align_bytes=64)
+            return csq
+
+        def multiply(block, csq, out):
+            ag_ps = psum_t.tile([P, PACK, P], F32)
+            for u in range(PACK):
+                nc.tensor.transpose(ag_ps[:, u, :], ag_of[block][:, u, :], ident_f32[:])
             nc.vector.scalar_tensor_tensor(
-                out=ds[:],
+                out=out,
                 in0=csq[:],
                 scalar=2.0,
                 in1=ag_ps[:].rearrange("i u b -> i b u"),
                 op0=ALU.mult,
                 op1=ALU.mult,
             )
-            return ds
-
-        def quantise(ds):
-            ds_codes = work.tile([P, P], U32, align_bytes=64)
-            ds_scales = work.tile([P, P], U8, align_bytes=64)
-            nc.vector.quantize_mx(
-                out=ds_codes[:].bitcast(E5M2_X4),
-                scales=ds_scales[:],
-                in_=ds[:].rearrange("i b u -> i (b u)"),
-            )
-            return ds_codes, ds_scales
 
         def products(block, ds_codes, ds_scales):
             o_sb = outs.tile([P, K], F32)
@@ -200,8 +200,8 @@ def tile_digitcaps_t_v_kernel(tc, x, W, s, grad_out, out):
                 o_ps = psum_o.tile([P, BANK], F32)
                 nc.tensor.matmul_mx(
                     out=o_ps[:],
-                    lhsT=ds_codes[:].bitcast(E5M2_X4),
-                    lhsT_scale=ds_scales[:],
+                    lhsT=ds_codes.bitcast(E5M2_X4),
+                    lhsT_scale=ds_scales,
                     rhs=w_codes[:, cols].bitcast(E4M3_X4),
                     rhs_scale=w_scales[:, cols],
                     start=True,
@@ -219,31 +219,57 @@ def tile_digitcaps_t_v_kernel(tc, x, W, s, grad_out, out):
                     nc.scalar.activation(
                         out=o_sb[:, cols], in_=o_ps[:], func=ACT.Copy, scale=1.0 / P
                     )
-                nc.sync.dma_start(out=out_rows[:, block, cols], in_=o_sb[:, cols])
+                if block >= BLOCKS - FINE_STORES:
+                    nc.sync.dma_start(out=out_rows[:, block, cols], in_=o_sb[:, cols])
+            if block < BLOCKS - FINE_STORES:
+                nc.sync.dma_start(out=out_rows[:, block, :], in_=o_sb[:])
 
         for kind, g in PHASE_1:
             if kind == "s":
-                magnitude(g)
-                logarithm(g)
+                magnitude(s_first[g], S_GROUPS[g])
+                logarithm(s_first[g], S_GROUPS[g])
             elif kind == "g":
-                times_grad(g)
-            elif kind == "w":
-                turn_w(nc, psum_o, w_sb, ident_f32, w_grouped, g)
+                times_grad(g_first[g], G_GROUPS[g])
+            elif kind == "r":
+                csq_of[g] = square(g)
+            elif kind == "h":
+                sigmoid(sig_first[g], SIG_GROUPS[g])
+            elif kind in "wx":
+                turn_w(nc, psum_o, w_sb, ident_f32, w_grouped, g, kind == "x")
             else:
                 quantise_w(nc, w_grouped, w_codes, w_scales)
 
-        c_of = {}
-        ds_of = {}
         codes = {}
         for step in range(BLOCKS + LAG):
-            if step < BLOCKS and step == first_block[group_of[step]]:
-                c_of[group_of[step]] = sigmoid(group_of[step])
-            if 0 <= step - 2 < BLOCKS:
-                g = group_of[step - 2]
-                ds_of[step - 2] = turn(g, step - 2 - first_block[g], c_of[g])
+            if not SQ_FIRST and step in sig_first and step not in c_of:
+                sigmoid(step, SIG_GROUPS[sig_first.index(step)])
+            block = step - LEAD
+            if 0 <= block < BLOCKS and block not in csq_of:
+                csq_of[block] = square(block)
+            if SQ_FIRST and step in sig_first and step not in c_of:
+                sigmoid(step, SIG_GROUPS[sig_first.index(step)])
+            block = step - LEAD - DEPTH
+            if 0 <= block < BLOCKS:
+                if QPAIR:
+                    if block % 2 == 0:
+                        ds = turns.tile([P, 2, P, PACK], BF16, tag="turn", align_bytes=64)
+                    multiply(block, csq_of[block], ds[:, block % 2, :, :])
+                else:
+                    ds = turns.tile([P, 1, P, PACK], BF16, tag="turn", align_bytes=64)
+                    multiply(block, csq_of[block], ds[:, 0, :, :])
             if step >= LAG:
                 products(step - LAG, codes[step - LAG][0], codes[step - LAG][1])
-            if 0 <= step - 2 < BLOCKS:
-                codes[step - 2] = quantise(ds_of[step - 2])
-                if first_block[V_GRADS] <= step - 2 + G_AHEAD < BLOCKS:
-                    times_grad_block(step - 2 + G_AHEAD)
+            if 0 <= block < BLOCKS:
+                if not QPAIR or block % 2 == 1:
+                    n = 2 if QPAIR else 1
+                    ds_codes = work.tile([P, n, P], U32, align_bytes=64)
+                    ds_scales = work.tile([P, n, P], U8, align_bytes=64)
+                    nc.vector.quantize_mx(
+                        out=ds_codes[:].rearrange("p t b -> p (t b)").bitcast(E5M2_X4),
+                        scales=ds_scales[:].rearrange("p t b -> p (t b)"),
+                        in_=ds[:].rearrange("i t b u -> i (t b u)"),
+                    )
+                    for t in range(n):
+                        codes[block - n + 1 + t] = (ds_codes[:, t, :], ds_scales[:, t, :])
+                if V_GRADS <= block + G_AHEAD < BLOCKS:
+                    times_grad_block(block + G_AHEAD)

@@ -23,15 +23,16 @@ G_GROUPS = (1, 1, 2, 2, 2, 2, 2, 2, 1, 1)
 SIG_GROUPS = (1, 1, 2, 2, 2, 2, 2, 2, 1, 1)
 LOADS = [("s", 0), ("s", 1), ("s", 2), ("s", 3), ("s", 4), ("s", 5), ("s", 6), ("s", 7), ("s", 8), ("s", 9), ("g", 0), ("g", 1), ("w", 0), ("g", 2), ("g", 3), ("g", 4), ("g", 5), ("g", 6), ("g", 7), ("g", 8), ("g", 9)]
 PHASE_1 = [("s", 0), ("s", 1), ("s", 2), ("s", 3), ("s", 4), ("s", 5), ("s", 6), ("s", 7), ("s", 8), ("s", 9), ("g", 0), ("g", 1), ("h", 0), ("h", 1), ("x", 0), ("w", 1), ("x", 2), ("w", 3), ("q", 0)]
-V_BOTH = (1, 3)
-S_BOTH = ()
-FINE_STORES = 8
+V_BOTH = (0, 2)
+S_BOTH = (11, 13, 15)
+FINE_STORES = 6
 V_GRADS = 2
 G_AHEAD = 2
 LEAD = 2
 DEPTH = 2
 LAG = 6
 QPAIR = False
+V_LATE = ()
 SQ_FIRST = False
 BANK = 512
 HALVES = K // BANK
@@ -122,6 +123,12 @@ def tile_digitcaps_t_v_kernel(tc, x, W, s, grad_out, out):
                 op0=ALU.bitwise_and,
             )
 
+        def cap(first, size):
+            flat = a_sb[:, first : first + size, :].rearrange("p t n -> p (t n)").bitcast(F32)
+            nc.vector.tensor_scalar(
+                out=flat, in0=flat, scalar1=2.0**40, scalar2=None, op0=ALU.min
+            )
+
         def logarithm(first, size):
             blocks = slice(first, first + size)
             nc.scalar.activation(
@@ -147,6 +154,17 @@ def tile_digitcaps_t_v_kernel(tc, x, W, s, grad_out, out):
 
         def times_grad_block(block):
             ag = turns.tile([P, PACK, P], F32, tag="turn", align_bytes=64)
+            if block in V_LATE:
+                nc.vector.scalar_tensor_tensor(
+                    out=ag[:].rearrange("p u i -> p (u i)"),
+                    in0=a_sb[:, block, :].bitcast(F32),
+                    scalar=2.0**40,
+                    in1=g_sb[:, block, :],
+                    op0=ALU.min,
+                    op1=ALU.mult,
+                )
+                ag_of[block] = ag[:]
+                return
             nc.gpsimd.tensor_tensor(
                 out=ag[:].rearrange("p u i -> p (u i)"),
                 in0=a_sb[:, block, :].bitcast(F32),
@@ -228,6 +246,8 @@ def tile_digitcaps_t_v_kernel(tc, x, W, s, grad_out, out):
             if kind == "s":
                 magnitude(s_first[g], S_GROUPS[g])
                 logarithm(s_first[g], S_GROUPS[g])
+            elif kind == "c":
+                cap(s_first[g], S_GROUPS[g])
             elif kind == "g":
                 times_grad(g_first[g], G_GROUPS[g])
             elif kind == "r":
@@ -240,6 +260,8 @@ def tile_digitcaps_t_v_kernel(tc, x, W, s, grad_out, out):
                 quantise_w(nc, w_grouped, w_codes, w_scales)
 
         codes = {}
+        for block in range(V_GRADS, G_AHEAD):
+            times_grad_block(block)
         for step in range(BLOCKS + LAG):
             if not SQ_FIRST and step in sig_first and step not in c_of:
                 sigmoid(step, SIG_GROUPS[sig_first.index(step)])

import concourse.mybir as mybir
from concourse.masks import make_identity

F32 = mybir.dt.float32
BF16 = mybir.dt.bfloat16
U32 = mybir.dt.uint32
I32 = mybir.dt.int32
U8 = mybir.dt.uint8
E4M3_X4 = mybir.dt.float8_e4m3fn_x4
E5M2_X4 = mybir.dt.float8_e5m2_x4
ACT = mybir.ActivationFunctionType
ALU = mybir.AluOpType

P = 128
PACK = 4
ROWS = 2048
N = 512
K = 1024
E_PAIRS = 4
BLOCKS = ROWS // P
S_GROUPS = (1, 1, 2, 2, 2, 2, 2, 2, 1, 1)
G_GROUPS = (1, 1, 2, 2, 2, 2, 2, 2, 1, 1)
SIG_GROUPS = (1, 1, 2, 2, 2, 2, 2, 2, 1, 1)
LOADS = [("s", 0), ("s", 1), ("s", 2), ("s", 3), ("s", 4), ("s", 5), ("s", 6), ("s", 7), ("s", 8), ("s", 9), ("g", 0), ("g", 1), ("w", 0), ("g", 2), ("g", 3), ("g", 4), ("g", 5), ("g", 6), ("g", 7), ("g", 8), ("g", 9)]
PHASE_1 = [("s", 0), ("s", 1), ("s", 2), ("s", 3), ("s", 4), ("s", 5), ("s", 6), ("s", 7), ("s", 8), ("s", 9), ("g", 0), ("g", 1), ("h", 0), ("h", 1), ("x", 0), ("w", 1), ("x", 2), ("w", 3), ("q", 0)]
V_BOTH = (0, 2)
S_BOTH = (11, 13, 15)
FINE_STORES = 6
V_GRADS = 2
G_AHEAD = 2
LEAD = 2
DEPTH = 2
LAG = 6
QPAIR = False
V_LATE = ()
SQ_FIRST = False
BANK = 512
HALVES = K // BANK

FLOPS = 2 * ROWS * K * N
BYTES = 2 * K * N + 4 * ROWS * N + 2 * ROWS * N + 4 * ROWS * K


def turn_w(nc, psum, w_sb, ident_f32, w_grouped, w, scalar):
    w_words = w_sb[:].bitcast(F32).rearrange("p (u i w) -> p u i w", u=PACK, i=P, w=E_PAIRS)
    w_ps = psum.tile([P, PACK, P], F32, tag="o_ps")
    for u in range(PACK):
        nc.tensor.transpose(w_ps[:, u, :], w_words[:, u, :, w], ident_f32[:])
    out = w_grouped[:, :, w, :, :]
    in_ = w_ps[:].bitcast(BF16).rearrange("i u (p l) -> i p l u", l=2)
    if scalar:
        nc.scalar.copy(out=out, in_=in_)
    else:
        nc.vector.tensor_copy(out=out, in_=in_)


def quantise_w(nc, w_grouped, w_codes, w_scales):
    w_flat = w_grouped[:].rearrange("i p w l u -> i (p w l u)")
    for h in range(HALVES):
        nc.vector.quantize_mx(
            out=w_codes[:, h * BANK : (h + 1) * BANK].bitcast(E4M3_X4),
            scales=w_scales[:, h * BANK : (h + 1) * BANK],
            in_=w_flat[:, h * BANK * PACK : (h + 1) * BANK * PACK],
        )


def tile_digitcaps_t_v_kernel(tc, x, W, s, grad_out, out):
    nc = tc.nc
    assert sum(S_GROUPS) == sum(G_GROUPS) == sum(SIG_GROUPS) == BLOCKS
    s_first = [sum(S_GROUPS[:g]) for g in range(len(S_GROUPS))]
    g_first = [sum(G_GROUPS[:g]) for g in range(len(G_GROUPS))]
    sig_first = [sum(SIG_GROUPS[:g]) for g in range(len(SIG_GROUPS))]
    s_rows = s.rearrange("(p t) c d -> p t (c d)", t=BLOCKS)
    g_rows = grad_out.rearrange("(p t) c d o -> p t (c d o)", t=BLOCKS)
    out_rows = out.rearrange("(p t) q e -> p t (q e)", t=BLOCKS)
    w_rows = W.rearrange("o p c d e -> (o p) (c d e)")

    with (
        tc.tile_pool(name="const", bufs=1) as const,
        tc.tile_pool(name="work", bufs=6) as work,
        tc.tile_pool(name="ahead", bufs=4) as ahead,
        tc.tile_pool(name="squares", bufs=10) as squares,
        tc.tile_pool(name="turns", bufs=5) as turns,
        tc.tile_pool(name="outs", bufs=4) as outs,
        tc.psum_pool(name="psum_t", bufs=2) as psum_t,
        tc.psum_pool(name="psum_o", bufs=4) as psum_o,
        tc.manual_schedule(engines={mybir.EngineType.Activation, mybir.EngineType.DVE}),
    ):
        s_sb = const.tile([P, BLOCKS, N], F32)
        a_sb = const.tile([P, BLOCKS, N], I32)
        g_sb = const.tile([P, BLOCKS, N], BF16)
        ag_sb = const.tile([P, max(V_GRADS, 1), PACK, P], F32)
        w_sb = const.tile([P, N * 8], BF16)

        for kind, g in LOADS:
            if kind == "w":
                nc.sync.dma_start(out=w_sb[:], in_=w_rows)
            elif kind == "s":
                blocks = slice(s_first[g], s_first[g] + S_GROUPS[g])
                nc.sync.dma_start(out=s_sb[:, blocks, :], in_=s_rows[:, blocks, :])
            else:
                blocks = slice(g_first[g], g_first[g] + G_GROUPS[g])
                nc.sync.dma_start(out=g_sb[:, blocks, :], in_=g_rows[:, blocks, :])

        ident_f32 = const.tile([P, P], F32)
        make_identity(nc, ident_f32[:])
        one = const.tile([P, 1], F32)
        nc.vector.memset(one[:], 1.0)
        warm = const.tile([P, 1], F32)
        nc.scalar.activation(out=warm[:], in_=one[:], func=ACT.Ln)

        w_codes = const.tile([P, K], U32, align_bytes=64)
        w_scales = const.tile([P, K], U8, align_bytes=64)
        w_grouped = const.tile([P, P, E_PAIRS, 2, PACK], BF16, align_bytes=64)

        def magnitude(first, size):
            blocks = slice(first, first + size)
            nc.vector.tensor_scalar(
                out=a_sb[:, blocks, :].rearrange("p t n -> p (t n)"),
                in0=s_sb[:, blocks, :].rearrange("p t n -> p (t n)").bitcast(I32),
                scalar1=0x7FFFFFFF,
                scalar2=None,
                op0=ALU.bitwise_and,
            )

        def cap(first, size):
            flat = a_sb[:, first : first + size, :].rearrange("p t n -> p (t n)").bitcast(F32)
            nc.vector.tensor_scalar(
                out=flat, in0=flat, scalar1=2.0**40, scalar2=None, op0=ALU.min
            )

        def logarithm(first, size):
            blocks = slice(first, first + size)
            nc.scalar.activation(
                out=s_sb[:, blocks, :].rearrange("p t n -> p (t n)"),
                in_=a_sb[:, blocks, :].rearrange("p t n -> p (t n)").bitcast(F32),
                func=ACT.Ln,
            )

        def times_grad(first, size):
            blocks = slice(first, first + size)
            nc.vector.scalar_tensor_tensor(
                out=ag_sb[:, blocks, :, :].rearrange("p t u i -> p (t u i)"),
                in0=a_sb[:, blocks, :].rearrange("p t n -> p (t n)").bitcast(F32),
                scalar=2.0**40,
                in1=g_sb[:, blocks, :].rearrange("p t n -> p (t n)"),
                op0=ALU.min,
                op1=ALU.mult,
            )

        ag_of = {}
        for block in range(V_GRADS):
            ag_of[block] = ag_sb[:, block, :, :]

        def times_grad_block(block):
            ag = turns.tile([P, PACK, P], F32, tag="turn", align_bytes=64)
            if block in V_LATE:
                nc.vector.scalar_tensor_tensor(
                    out=ag[:].rearrange("p u i -> p (u i)"),
                    in0=a_sb[:, block, :].bitcast(F32),
                    scalar=2.0**40,
                    in1=g_sb[:, block, :],
                    op0=ALU.min,
                    op1=ALU.mult,
                )
                ag_of[block] = ag[:]
                return
            nc.gpsimd.tensor_tensor(
                out=ag[:].rearrange("p u i -> p (u i)"),
                in0=a_sb[:, block, :].bitcast(F32),
                in1=g_sb[:, block, :],
                op=ALU.mult,
            )
            ag_of[block] = ag[:]

        c_of = {}
        csq_of = {}

        def sigmoid(first, size):
            blocks = slice(first, first + size)
            c = ahead.tile([P, size, PACK, P], F32)
            nc.scalar.activation(
                out=c[:].rearrange("p t u i -> p (t u i)"),
                in_=s_sb[:, blocks, :].rearrange("p t n -> p (t n)"),
                func=ACT.Sigmoid,
                scale=-2.0,
            )
            for t in range(size):
                c_of[first + t] = c[:, t, :, :]

        def square(block):
            c_ps = psum_t.tile([P, PACK, P], F32)
            for u in range(PACK):
                nc.tensor.transpose(c_ps[:, u, :], c_of[block][:, u, :], ident_f32[:])
            csq = squares.tile([P, P, PACK], F32)
            nc.scalar.activation(
                out=csq[:], in_=c_ps[:].rearrange("i u b -> i b u"), func=ACT.Square
            )
            return csq

        def multiply(block, csq, out):
            ag_ps = psum_t.tile([P, PACK, P], F32)
            for u in range(PACK):
                nc.tensor.transpose(ag_ps[:, u, :], ag_of[block][:, u, :], ident_f32[:])
            nc.vector.scalar_tensor_tensor(
                out=out,
                in0=csq[:],
                scalar=2.0,
                in1=ag_ps[:].rearrange("i u b -> i b u"),
                op0=ALU.mult,
                op1=ALU.mult,
            )

        def products(block, ds_codes, ds_scales):
            o_sb = outs.tile([P, K], F32)
            for h in range(HALVES):
                cols = slice(h * BANK, (h + 1) * BANK)
                o_ps = psum_o.tile([P, BANK], F32)
                nc.tensor.matmul_mx(
                    out=o_ps[:],
                    lhsT=ds_codes.bitcast(E5M2_X4),
                    lhsT_scale=ds_scales,
                    rhs=w_codes[:, cols].bitcast(E4M3_X4),
                    rhs_scale=w_scales[:, cols],
                    start=True,
                    stop=True,
                )
                if (h == HALVES - 1 and block not in S_BOTH) or block in V_BOTH:
                    nc.vector.tensor_scalar(
                        out=o_sb[:, cols],
                        in0=o_ps[:],
                        scalar1=1.0 / P,
                        scalar2=None,
                        op0=ALU.mult,
                    )
                else:
                    nc.scalar.activation(
                        out=o_sb[:, cols], in_=o_ps[:], func=ACT.Copy, scale=1.0 / P
                    )
                if block >= BLOCKS - FINE_STORES:
                    nc.sync.dma_start(out=out_rows[:, block, cols], in_=o_sb[:, cols])
            if block < BLOCKS - FINE_STORES:
                nc.sync.dma_start(out=out_rows[:, block, :], in_=o_sb[:])

        for kind, g in PHASE_1:
            if kind == "s":
                magnitude(s_first[g], S_GROUPS[g])
                logarithm(s_first[g], S_GROUPS[g])
            elif kind == "c":
                cap(s_first[g], S_GROUPS[g])
            elif kind == "g":
                times_grad(g_first[g], G_GROUPS[g])
            elif kind == "r":
                csq_of[g] = square(g)
            elif kind == "h":
                sigmoid(sig_first[g], SIG_GROUPS[g])
            elif kind in "wx":
                turn_w(nc, psum_o, w_sb, ident_f32, w_grouped, g, kind == "x")
            else:
                quantise_w(nc, w_grouped, w_codes, w_scales)

        codes = {}
        for block in range(V_GRADS, G_AHEAD):
            times_grad_block(block)
        for step in range(BLOCKS + LAG):
            if not SQ_FIRST and step in sig_first and step not in c_of:
                sigmoid(step, SIG_GROUPS[sig_first.index(step)])
            block = step - LEAD
            if 0 <= block < BLOCKS and block not in csq_of:
                csq_of[block] = square(block)
            if SQ_FIRST and step in sig_first and step not in c_of:
                sigmoid(step, SIG_GROUPS[sig_first.index(step)])
            block = step - LEAD - DEPTH
            if 0 <= block < BLOCKS:
                if QPAIR:
                    if block % 2 == 0:
                        ds = turns.tile([P, 2, P, PACK], BF16, tag="turn", align_bytes=64)
                    multiply(block, csq_of[block], ds[:, block % 2, :, :])
                else:
                    ds = turns.tile([P, 1, P, PACK], BF16, tag="turn", align_bytes=64)
                    multiply(block, csq_of[block], ds[:, 0, :, :])
            if step >= LAG:
                products(step - LAG, codes[step - LAG][0], codes[step - LAG][1])
            if 0 <= block < BLOCKS:
                if not QPAIR or block % 2 == 1:
                    n = 2 if QPAIR else 1
                    ds_codes = work.tile([P, n, P], U32, align_bytes=64)
                    ds_scales = work.tile([P, n, P], U8, align_bytes=64)
                    nc.vector.quantize_mx(
                        out=ds_codes[:].rearrange("p t b -> p (t b)").bitcast(E5M2_X4),
                        scales=ds_scales[:].rearrange("p t b -> p (t b)"),
                        in_=ds[:].rearrange("i t b u -> i (t b u)"),
                    )
                    for t in range(n):
                        codes[block - n + 1 + t] = (ds_codes[:, t, :], ds_scales[:, t, :])
                if V_GRADS <= block + G_AHEAD < BLOCKS:
                    times_grad_block(block + G_AHEAD)
